import numpy as np
import ml_dtypes


def mxq(x, axis, fmt="e4m3"):
    dtype, down = {"e4m3": (ml_dtypes.float8_e4m3fn, 7), "e5m2": (ml_dtypes.float8_e5m2, 14)}[fmt]
    v = np.moveaxis(np.asarray(x, np.float32).astype(ml_dtypes.bfloat16).astype(np.float64), axis, -1)
    blocks = v.reshape(v.shape[:-1] + (-1, 32))
    amax = np.abs(blocks).max(-1, keepdims=True)
    byte = np.maximum(np.where(amax > 0, np.frexp(amax)[1] - 1 + 127, 0) - down, 1)
    scale = np.exp2(byte - 127.0)
    codes = (blocks / scale).astype(np.float32).astype(dtype).astype(np.float64)
    return np.moveaxis((codes * scale).reshape(v.shape), -1, axis)


WIDE = False


def mx_kscale(k):
    if not WIDE:
        return np.ones(k)
    levels = np.array([10, -10, 5, -5, 0])
    if k % 512:
        return np.exp2(np.random.permutation(np.resize(levels, k // 32))).repeat(32)
    a = np.empty((k // 512, 16))
    for p in range(k // 512):
        a[p, :8] = np.random.permutation(np.resize(levels, 8))
        for g in range(8):
            far = levels[np.abs(levels - a[p, g]) >= 10]
            a[p, g + 8] = far[np.random.randint(len(far))]
    return np.exp2(a.ravel()).repeat(32)


BF16 = ml_dtypes.bfloat16


def bf(x):
    return np.asarray(x, np.float32).astype(BF16)


def f64(x):
    return np.asarray(x).astype(np.float64)


B, N, D_IN, H, D_HEAD, D_EXPAND = 8, 1024, 512, 1, 64, 2048
D_Q = D_HEAD * H
D_V = D_IN * H
D_QKV = 2 * D_Q + D_V
EPS = 1e-5


def feature_norm(x, gamma, beta):
    mean = x.mean(axis=1, keepdims=True)
    var = x.var(axis=1, keepdims=True)
    return gamma * (x - mean) / np.sqrt(var + EPS) + beta


def sigmoid(v):
    e = np.exp(-np.abs(v))
    return np.where(v >= 0.0, 1.0, e) / (1.0 + e)


def swish(v):
    return v * sigmoid(v)


def setup_inputs():
    wcol = np.concatenate([np.full(2 * D_Q, 1.9 / np.sqrt(D_HEAD * D_IN)), np.full(D_V, 0.5 / np.sqrt(D_IN))])
    bcol = np.concatenate([np.full(2 * D_Q, 0.03), np.full(D_V, 0.1)])
    s = mx_kscale(D_IN)
    t = s / s.min()
    return {"x": bf(1.5 * np.random.standard_normal((B, N, D_IN)) + 0.5 * np.random.standard_normal((1, 1, D_IN))),
            "pos_enc": bf(np.random.standard_normal((1, N, D_IN)) * t),
            "gamma1": bf((1.0 + 0.1 * np.random.standard_normal((1, 1, D_IN))) * t),
            "beta1": bf(0.1 * np.random.standard_normal((1, 1, D_IN)) * t),
            "W_qkv": bf(np.random.standard_normal((D_IN, D_QKV)) * wcol / t[:, None]),
            "b_qkv": bf(np.random.standard_normal(D_QKV) * bcol)}


def reference(x, pos_enc, gamma1, beta1, W_qkv, b_qkv):
    h = feature_norm(f64(x), f64(gamma1), f64(beta1)) + f64(pos_enc)
    a = swish(h)
    return (mxq(a, 2, "e4m3") @ mxq(f64(W_qkv), 0, "e4m3")) + f64(b_qkv)

@@ -1,0 +1,286 @@
+from contextlib import ExitStack
+
+import concourse.masks as masks
+import concourse.mybir as mybir
+
+F32 = mybir.dt.float32
+BF16 = mybir.dt.bfloat16
+U32 = mybir.dt.uint32
+U8 = mybir.dt.uint8
+FP8X4 = mybir.dt.float8_e4m3fn_x4
+ACT = mybir.ActivationFunctionType
+ALU = mybir.AluOpType
+
+P = 128
+PACK = 4
+BATCH = 8
+TOKENS = 1024
+D_IN = P * PACK
+D_OUT = 640
+TILES = TOKENS // P
+HALF_TILES = TILES // 2
+HALF = TOKENS // 2
+PAIR = PACK // 2
+WIDE = 512
+NARROW = D_OUT - WIDE
+BANKS_PER_HALF = 1 + HALF_TILES
+FILLS = 2 * BANKS_PER_HALF
+AHEAD = 3
+STORE_TILES = 2
+EPS = 1e-5
+
+FLOPS = 2 * BATCH * TOKENS * D_IN * D_OUT
+
+
+def tile_attentionblock_pa_t_kernel(tc, x, pos_enc, gamma1, beta1, W_qkv, b_qkv, out):
+    nc = tc.nc
+    with ExitStack() as ctx:
+        const = ctx.enter_context(tc.tile_pool(name="const", bufs=1))
+        work = ctx.enter_context(tc.tile_pool(name="work", bufs=2))
+        small = ctx.enter_context(tc.tile_pool(name="small", bufs=4))
+        psum = ctx.enter_context(tc.psum_pool(name="psum", bufs=1))
+        ctx.enter_context(tc.manual_schedule())
+
+        gamma = const.tile([P, PACK], BF16)
+        beta = const.tile([P, PACK], BF16)
+
+        x_nat = {}
+
+        def load_x(b):
+            x_nat[b] = const.tile([P, TILES, D_IN], BF16, name="x%d" % b)
+            nc.sync.dma_start(out=x_nat[b][:], in_=x[b, :, :].rearrange("(p j) d -> p j d", j=TILES))
+
+        load_x(0)
+        nc.sync.dma_start(out=gamma[:], in_=gamma1[0, :, :].rearrange("a (p t) -> (a p) t", t=PACK))
+        nc.sync.dma_start(out=beta[:], in_=beta1[0, :, :].rearrange("a (p t) -> (a p) t", t=PACK))
+        pos_nat = const.tile([P, TILES, D_IN], BF16)
+        nc.sync.dma_start(out=pos_nat[:], in_=pos_enc[0, :, :].rearrange("(p j) d -> p j d", j=TILES))
+        load_x(1)
+        w_raw = const.tile([P, PACK, D_OUT], BF16)
+        nc.sync.dma_start(out=w_raw[:], in_=W_qkv.rearrange("(p t) n -> p t n", t=PACK))
+        bias_bc = const.tile([P, D_OUT], BF16)
+        nc.sync.dma_start(out=bias_bc[:], in_=b_qkv.partition_broadcast(P))
+        for b in range(2, BATCH):
+            load_x(b)
+
+        ident = const.tile([P, P], BF16)
+        masks.make_identity(nc, ident[:])
+        ones = const.tile([P, 1], BF16)
+        nc.vector.memset(ones[:], 1.0)
+        minus_half = const.tile([P, PAIR], F32)
+        nc.vector.memset(minus_half[:], -0.5)
+        warm = const.tile([P, 1], F32)
+        nc.vector.memset(warm[:], 0.0)
+        nc.scalar.activation(out=warm[:], in_=warm[:], func=ACT.Silu)
+
+        neg_mean, sum_sq, var_eps, scale, shift = {}, {}, {}, {}, {}
+        x_t, h_pl, a_pl, a_grp, a_codes, a_scales = {}, {}, {}, {}, {}, {}
+        prod, out_sb = {}, {}
+
+        def token_sums(b):
+            sums = psum.tile([P, PACK], F32, name="sums")
+            for t in range(PACK):
+                for j in range(TILES):
+                    nc.tensor.matmul(
+                        out=sums[:, t : t + 1],
+                        lhsT=x_nat[b][:, j, t:D_IN:PACK],
+                        rhs=ones[:],
+                        start=(j == 0),
+                        stop=(j == TILES - 1),
+                    )
+            neg_mean[b] = small.tile([P, PACK], F32, name="neg_mean")
+            nc.scalar.activation(out=neg_mean[b][:], in_=sums[:], func=ACT.Copy, scale=-1.0 / TOKENS)
+            sum_sq[b] = small.tile([P, PACK], F32, name="sum_sq")
+            var_eps[b] = small.tile([P, PACK], F32, name="var_eps")
+            scale[b] = small.tile([P, PACK], F32, name="scale")
+            shift[b] = small.tile([P, PACK], F32, name="shift")
+
+        def transpose_plane(b, t):
+            x_t[b, t] = psum.tile([P, TOKENS], BF16, name="x_t", tag="x_t%d" % t)
+            for j in range(TILES):
+                nc.tensor.transpose(x_t[b, t][:, j * P : (j + 1) * P], x_nat[b][:, j, t:D_IN:PACK], ident[:])
+
+        def centred_squares(b, t):
+            unused = work.tile([P, TOKENS], BF16, name="unused")
+            nc.scalar.activation(
+                out=unused[:],
+                in_=x_t[b, t][:],
+                func=ACT.Square,
+                bias=neg_mean[b][:, t : t + 1],
+                scale=1.0,
+                accum_out=sum_sq[b][:, t : t + 1],
+            )
+
+        def scale_of(b, pair):
+            planes = slice(pair * PAIR, (pair + 1) * PAIR)
+            nc.gpsimd.tensor_scalar(
+                out=var_eps[b][:, planes],
+                in0=sum_sq[b][:, planes],
+                scalar1=1.0 / TOKENS,
+                scalar2=EPS,
+                op0=ALU.mult,
+                op1=ALU.add,
+            )
+            rstd = small.tile([P, PAIR], F32, name="rstd")
+            nc.gpsimd.tensor_tensor(out=rstd[:], in0=var_eps[b][:, planes], in1=minus_half[:], op=ALU.pow)
+            nc.gpsimd.tensor_tensor(out=scale[b][:, planes], in0=rstd[:], in1=gamma[:, planes], op=ALU.mult)
+
+        def shift_of(b):
+            moved = small.tile([P, PACK], F32, name="moved")
+            nc.gpsimd.tensor_tensor(out=moved[:], in0=neg_mean[b][:], in1=scale[b][:], op=ALU.mult)
+            nc.gpsimd.tensor_tensor(out=shift[b][:], in0=moved[:], in1=beta[:], op=ALU.add)
+
+        def normalise_plane(b, t):
+            if t == 0:
+                h_pl[b] = work.tile([P, PACK, TOKENS], F32, name="h_pl")
+            nc.vector.scalar_tensor_tensor(
+                out=h_pl[b][:, t, :],
+                in0=x_t[b, t][:],
+                scalar=scale[b][:, t : t + 1],
+                in1=pos_t[:, t, :],
+                op0=ALU.mult,
+                op1=ALU.add,
+            )
+
+        def swish(b):
+            a_pl[b] = work.tile([P, PACK, TOKENS], BF16, name="a_pl")
+            for t in range(PACK):
+                nc.scalar.activation(
+                    out=a_pl[b][:, t, :], in_=h_pl[b][:, t, :], func=ACT.Silu, bias=shift[b][:, t : t + 1], scale=1.0
+                )
+
+        def regroup(b, half):
+            if half == 0:
+                a_grp[b] = work.tile([P, TOKENS, PACK], BF16, name="a_grp", align_bytes=64)
+            cols = slice(half * HALF, (half + 1) * HALF)
+            nc.gpsimd.tensor_scalar(
+                out=a_grp[b][:, cols, :],
+                in0=a_pl[b][:, :, cols].rearrange("p t w -> p w t"),
+                scalar1=1.0,
+                scalar2=0.0,
+                op0=ALU.mult,
+                op1=ALU.add,
+            )
+
+        def quantise(b, half):
+            if half == 0:
+                a_codes[b] = work.tile([P, TOKENS], U32, name="a_codes", align_bytes=64)
+                a_scales[b] = work.tile([P, TOKENS], U8, name="a_scales", align_bytes=64)
+            cols = slice(half * HALF, (half + 1) * HALF)
+            nc.vector.quantize_mx(
+                out=a_codes[b][:, cols].bitcast(FP8X4),
+                scales=a_scales[b][:, cols],
+                in_=a_grp[b][:, cols, :].rearrange("p w t -> p (w t)"),
+            )
+
+        def multiply(b, j, acc, w_cols):
+            tokens = slice(j * P, (j + 1) * P)
+            nc.tensor.matmul_mx(
+                out=acc,
+                lhsT=a_codes[b][:, tokens].bitcast(FP8X4),
+                lhsT_scale=a_scales[b][:, tokens],
+                rhs=w_codes[:, w_cols].bitcast(FP8X4),
+                rhs_scale=w_scales[:, w_cols],
+                start=True,
+                stop=True,
+            )
+
+        def fill(b, k):
+            half, i = divmod(k, BANKS_PER_HALF)
+            prod[b, k] = psum.tile([P, WIDE], F32, name="prod", bufs=AHEAD)
+            if i == 0:
+                for n in range(HALF_TILES):
+                    multiply(b, half * HALF_TILES + n, prod[b, k][:, n * NARROW : (n + 1) * NARROW], slice(WIDE, D_OUT))
+            else:
+                multiply(b, half * HALF_TILES + i - 1, prod[b, k][:], slice(0, WIDE))
+
+        def drain(b, k):
+            half, i = divmod(k, BANKS_PER_HALF)
+            if i == 0:
+                tiles = slice(half * HALF_TILES, (half + 1) * HALF_TILES)
+                nc.vector.tensor_tensor(
+                    out=out_sb[b][:, tiles, WIDE:D_OUT],
+                    in0=prod[b, k][:].rearrange("p (n c) -> p n c", c=NARROW),
+                    in1=bias_bc[:, WIDE:D_OUT].unsqueeze(1).to_broadcast([P, HALF_TILES, NARROW]),
+                    op=ALU.add,
+                )
+            else:
+                j = half * HALF_TILES + i - 1
+                nc.vector.tensor_tensor(out=out_sb[b][:, j, 0:WIDE], in0=prod[b, k][:], in1=bias_bc[:, 0:WIDE], op=ALU.add)
+                if j % STORE_TILES == STORE_TILES - 1:
+                    done = slice(j + 1 - STORE_TILES, j + 1)
+                    nc.sync.dma_start(
+                        out=out[b, :, :].rearrange("(p j) c -> p j c", j=TILES)[:, done, :], in_=out_sb[b][:, done, :]
+                    )
+
+        def finish(b, half):
+            if half == 0:
+                out_sb[b] = work.tile([P, TILES, D_OUT], F32, name="out_sb")
+            for k in range(half * BANKS_PER_HALF, (half + 1) * BANKS_PER_HALF):
+                drain(b, k)
+                if k + AHEAD < FILLS:
+                    fill(b, k + AHEAD)
+
+        def statistics(b, pair):
+            for t in range(pair * PAIR, (pair + 1) * PAIR):
+                transpose_plane(b, t)
+                centred_squares(b, t)
+            scale_of(b, pair)
+
+        token_sums(0)
+        for pair in range(2):
+            statistics(0, pair)
+        shift_of(0)
+
+        pos_t = const.tile([P, PACK, TOKENS], BF16)
+        for t in range(PACK):
+            pos_ps = psum.tile([P, TOKENS], BF16, name="pos_ps", tag="prod", bufs=AHEAD)
+            for j in range(TILES):
+                nc.tensor.transpose(pos_ps[:, j * P : (j + 1) * P], pos_nat[:, j, t:D_IN:PACK], ident[:])
+            nc.vector.tensor_copy(out=pos_t[:, t, :], in_=pos_ps[:])
+        token_sums(1)
+
+        w_grp = const.tile([P, D_OUT, PACK], BF16, align_bytes=64)
+        w_codes = const.tile([P, D_OUT], U32, align_bytes=64)
+        w_scales = const.tile([P, D_OUT], U8, align_bytes=64)
+
+        def quantise_weights():
+            nc.vector.tensor_copy(out=w_grp[:], in_=w_raw[:].rearrange("p t n -> p n t"))
+            for w_cols in (slice(0, WIDE), slice(WIDE, D_OUT)):
+                nc.vector.quantize_mx(
+                    out=w_codes[:, w_cols].bitcast(FP8X4),
+                    scales=w_scales[:, w_cols],
+                    in_=w_grp[:, w_cols, :].rearrange("p n t -> p (n t)"),
+                )
+
+        for b in range(BATCH + 2):
+            for pair in range(2):
+                for t in range(pair * PAIR, (pair + 1) * PAIR):
+                    if b < BATCH:
+                        normalise_plane(b, t)
+                    if b + 1 < BATCH:
+                        transpose_plane(b + 1, t)
+                        centred_squares(b + 1, t)
+                if b + 1 < BATCH:
+                    scale_of(b + 1, pair)
+            if b + 1 < BATCH:
+                shift_of(b + 1)
+            if b < BATCH:
+                swish(b)
+            if b >= 2:
+                finish(b - 2, 0)
+            if b == 1:
+                quantise_weights()
+            if 1 <= b <= BATCH:
+                for half in range(2):
+                    quantise(b - 1, half)
+            if b >= 2:
+                finish(b - 2, 1)
+            if 1 <= b <= BATCH:
+                for k in range(AHEAD):
+                    fill(b - 1, k)
+            if b < BATCH:
+                for half in range(2):
+                    regroup(b, half)
+            if b + 2 < BATCH:
+                token_sums(b + 2)

@@ -25,6 +25,7 @@ WIDE = 512
 NARROW = D_OUT - WIDE
 BANKS_PER_HALF = 1 + HALF_TILES
 FILLS = 2 * BANKS_PER_HALF
+SUM_COLS = 48
 AHEAD = 3
 STORE_TILES = 2
 EPS = 1e-5
@@ -65,7 +66,7 @@ def tile_attentionblock_pa_t_kernel(tc, x, pos_enc, gamma1, beta1, W_qkv, b_qkv,
 
         ident = const.tile([P, P], BF16)
         masks.make_identity(nc, ident[:])
-        ones = const.tile([P, 1], BF16)
+        ones = const.tile([P, SUM_COLS], BF16)
         nc.vector.memset(ones[:], 1.0)
         minus_half = const.tile([P, PAIR], F32)
         nc.vector.memset(minus_half[:], -0.5)
@@ -73,23 +74,25 @@ def tile_attentionblock_pa_t_kernel(tc, x, pos_enc, gamma1, beta1, W_qkv, b_qkv,
         nc.vector.memset(warm[:], 0.0)
         nc.scalar.activation(out=warm[:], in_=warm[:], func=ACT.Silu)
 
-        neg_mean, sum_sq, var_eps, scale, shift = {}, {}, {}, {}, {}
+        sums, neg_mean, sum_sq, var_eps, scale, shift = {}, {}, {}, {}, {}, {}
         x_t, h_pl, a_pl, a_grp, a_codes, a_scales = {}, {}, {}, {}, {}, {}
         prod, out_sb = {}, {}
 
-        def token_sums(b):
-            sums = psum.tile([P, PACK], F32, name="sums")
-            for t in range(PACK):
-                for j in range(TILES):
-                    nc.tensor.matmul(
-                        out=sums[:, t : t + 1],
-                        lhsT=x_nat[b][:, j, t:D_IN:PACK],
-                        rhs=ones[:],
-                        start=(j == 0),
-                        stop=(j == TILES - 1),
-                    )
+        def token_sums(b, t):
+            if t == 0:
+                sums[b] = psum.tile([P, PACK, SUM_COLS], F32, name="sums")
+            for j in range(TILES):
+                nc.tensor.matmul(
+                    out=sums[b][:, t, :],
+                    lhsT=x_nat[b][:, j, t:D_IN:PACK],
+                    rhs=ones[:],
+                    start=(j == 0),
+                    stop=(j == TILES - 1),
+                )
+
+        def means(b):
             neg_mean[b] = small.tile([P, PACK], F32, name="neg_mean")
-            nc.scalar.activation(out=neg_mean[b][:], in_=sums[:], func=ACT.Copy, scale=-1.0 / TOKENS)
+            nc.scalar.activation(out=neg_mean[b][:], in_=sums[b][:, :, 0], func=ACT.Copy, scale=-1.0 / TOKENS)
             sum_sq[b] = small.tile([P, PACK], F32, name="sum_sq")
             var_eps[b] = small.tile([P, PACK], F32, name="var_eps")
             scale[b] = small.tile([P, PACK], F32, name="scale")
@@ -227,7 +230,9 @@ def tile_attentionblock_pa_t_kernel(tc, x, pos_enc, gamma1, beta1, W_qkv, b_qkv,
                 centred_squares(b, t)
             scale_of(b, pair)
 
-        token_sums(0)
+        for t in range(PACK):
+            token_sums(0, t)
+        means(0)
         for pair in range(2):
             statistics(0, pair)
         shift_of(0)
@@ -238,7 +243,9 @@ def tile_attentionblock_pa_t_kernel(tc, x, pos_enc, gamma1, beta1, W_qkv, b_qkv,
             for j in range(TILES):
                 nc.tensor.transpose(pos_ps[:, j * P : (j + 1) * P], pos_nat[:, j, t:D_IN:PACK], ident[:])
             nc.vector.tensor_copy(out=pos_t[:, t, :], in_=pos_ps[:])
-        token_sums(1)
+        for t in range(PACK):
+            token_sums(1, t)
+        means(1)
 
         w_grp = const.tile([P, D_OUT, PACK], BF16, align_bytes=64)
         w_codes = const.tile([P, D_OUT], U32, align_bytes=64)
@@ -261,6 +268,8 @@ def tile_attentionblock_pa_t_kernel(tc, x, pos_enc, gamma1, beta1, W_qkv, b_qkv,
                     if b + 1 < BATCH:
                         transpose_plane(b + 1, t)
                         centred_squares(b + 1, t)
+                    if b + 2 < BATCH:
+                        token_sums(b + 2, t)
                 if b + 1 < BATCH:
                     scale_of(b + 1, pair)
             if b + 1 < BATCH:
@@ -283,4 +292,4 @@ def tile_attentionblock_pa_t_kernel(tc, x, pos_enc, gamma1, beta1, W_qkv, b_qkv,
                 for half in range(2):
                     regroup(b, half)
             if b + 2 < BATCH:
-                token_sums(b + 2)
+                means(b + 2)

@@ -20,11 +20,13 @@ D_OUT = 640
 TILES = TOKENS // P
 HALF_TILES = TILES // 2
 HALF = TOKENS // 2
+QUARTERS = PACK
+PIECE = TOKENS // QUARTERS
 PAIR = PACK // 2
 WIDE = 512
 NARROW = D_OUT - WIDE
 BANKS_PER_HALF = 1 + HALF_TILES
-FILLS = 2 * BANKS_PER_HALF
+DRAIN_LAG = 7
 SUM_COLS = 48
 AHEAD = 3
 STORE_TILES = 2
@@ -116,22 +118,20 @@ def tile_attentionblock_pa_t_kernel(tc, x, pos_enc, gamma1, beta1, W_qkv, b_qkv,
 
         def scale_of(b, pair):
             planes = slice(pair * PAIR, (pair + 1) * PAIR)
-            nc.gpsimd.tensor_scalar(
-                out=var_eps[b][:, planes],
-                in0=sum_sq[b][:, planes],
-                scalar1=1.0 / TOKENS,
-                scalar2=EPS,
-                op0=ALU.mult,
-                op1=ALU.add,
-            )
+            nc.scalar.activation(out=var_eps[b][:, planes], in_=sum_sq[b][:, planes], func=ACT.Copy, scale=1.0 / TOKENS, bias=EPS)
             rstd = small.tile([P, PAIR], F32, name="rstd")
             nc.gpsimd.tensor_tensor(out=rstd[:], in0=var_eps[b][:, planes], in1=minus_half[:], op=ALU.pow)
             nc.gpsimd.tensor_tensor(out=scale[b][:, planes], in0=rstd[:], in1=gamma[:, planes], op=ALU.mult)
 
-        def shift_of(b):
-            moved = small.tile([P, PACK], F32, name="moved")
-            nc.gpsimd.tensor_tensor(out=moved[:], in0=neg_mean[b][:], in1=scale[b][:], op=ALU.mult)
-            nc.gpsimd.tensor_tensor(out=shift[b][:], in0=moved[:], in1=beta[:], op=ALU.add)
+        def shift_of(b, pair):
+            for t in range(pair * PAIR, (pair + 1) * PAIR):
+                nc.scalar.activation(
+                    out=shift[b][:, t : t + 1],
+                    in_=scale[b][:, t : t + 1],
+                    func=ACT.Identity,
+                    scale=neg_mean[b][:, t : t + 1],
+                    bias=beta[:, t : t + 1],
+                )
 
         def normalise_plane(b, t):
             if t == 0:
@@ -145,17 +145,17 @@ def tile_attentionblock_pa_t_kernel(tc, x, pos_enc, gamma1, beta1, W_qkv, b_qkv,
                 op1=ALU.add,
             )
 
-        def swish(b):
-            a_pl[b] = work.tile([P, PACK, TOKENS], BF16, name="a_pl")
-            for t in range(PACK):
-                nc.scalar.activation(
-                    out=a_pl[b][:, t, :], in_=h_pl[b][:, t, :], func=ACT.Silu, bias=shift[b][:, t : t + 1], scale=1.0
-                )
+        def swish(b, t):
+            if t == 0:
+                a_pl[b] = work.tile([P, PACK, TOKENS], BF16, name="a_pl")
+            nc.scalar.activation(
+                out=a_pl[b][:, t, :], in_=h_pl[b][:, t, :], func=ACT.Silu, bias=shift[b][:, t : t + 1], scale=1.0
+            )
 
-        def regroup(b, half):
-            if half == 0:
+        def regroup(b, piece):
+            if piece == 0:
                 a_grp[b] = work.tile([P, TOKENS, PACK], BF16, name="a_grp", align_bytes=64)
-            cols = slice(half * HALF, (half + 1) * HALF)
+            cols = slice(piece * PIECE, (piece + 1) * PIECE)
             nc.gpsimd.tensor_scalar(
                 out=a_grp[b][:, cols, :],
                 in0=a_pl[b][:, :, cols].rearrange("p t w -> p w t"),
@@ -188,54 +188,55 @@ def tile_attentionblock_pa_t_kernel(tc, x, pos_enc, gamma1, beta1, W_qkv, b_qkv,
                 stop=True,
             )
 
-        def fill(b, k):
-            half, i = divmod(k, BANKS_PER_HALF)
-            prod[b, k] = psum.tile([P, WIDE], F32, name="prod", bufs=AHEAD)
-            if i == 0:
-                for n in range(HALF_TILES):
-                    multiply(b, half * HALF_TILES + n, prod[b, k][:, n * NARROW : (n + 1) * NARROW], slice(WIDE, D_OUT))
-            else:
-                multiply(b, half * HALF_TILES + i - 1, prod[b, k][:], slice(0, WIDE))
+        to_fill, to_drain = [], []
 
-        def drain(b, k):
-            half, i = divmod(k, BANKS_PER_HALF)
+        def fill_free_banks():
+            while to_fill and len(to_drain) < AHEAD:
+                b, half, i = to_fill[0]
+                to_fill.remove(to_fill[0])
+                acc = psum.tile([P, WIDE], F32, name="prod", bufs=AHEAD)
+                if i == 0:
+                    for n in range(HALF_TILES):
+                        multiply(b, half * HALF_TILES + n, acc[:, n * NARROW : (n + 1) * NARROW], slice(WIDE, D_OUT))
+                else:
+                    multiply(b, half * HALF_TILES + i - 1, acc[:], slice(0, WIDE))
+                prod[b, half, i] = acc
+                to_drain.append((b, half, i))
+
+        def drain():
+            b, half, i = to_drain[0]
+            to_drain.remove(to_drain[0])
+            if half == 0 and i == 0:
+                out_sb[b] = work.tile([P, TILES, D_OUT], F32, name="out_sb")
             if i == 0:
                 tiles = slice(half * HALF_TILES, (half + 1) * HALF_TILES)
                 nc.vector.tensor_tensor(
                     out=out_sb[b][:, tiles, WIDE:D_OUT],
-                    in0=prod[b, k][:].rearrange("p (n c) -> p n c", c=NARROW),
+                    in0=prod[b, half, i][:].rearrange("p (n c) -> p n c", c=NARROW),
                     in1=bias_bc[:, WIDE:D_OUT].unsqueeze(1).to_broadcast([P, HALF_TILES, NARROW]),
                     op=ALU.add,
                 )
             else:
                 j = half * HALF_TILES + i - 1
-                nc.vector.tensor_tensor(out=out_sb[b][:, j, 0:WIDE], in0=prod[b, k][:], in1=bias_bc[:, 0:WIDE], op=ALU.add)
+                nc.vector.tensor_tensor(
+                    out=out_sb[b][:, j, 0:WIDE], in0=prod[b, half, i][:], in1=bias_bc[:, 0:WIDE], op=ALU.add
+                )
                 if j % STORE_TILES == STORE_TILES - 1:
                     done = slice(j + 1 - STORE_TILES, j + 1)
                     nc.sync.dma_start(
                         out=out[b, :, :].rearrange("(p j) c -> p j c", j=TILES)[:, done, :], in_=out_sb[b][:, done, :]
                     )
 
-        def finish(b, half):
-            if half == 0:
-                out_sb[b] = work.tile([P, TILES, D_OUT], F32, name="out_sb")
-            for k in range(half * BANKS_PER_HALF, (half + 1) * BANKS_PER_HALF):
-                drain(b, k)
-                if k + AHEAD < FILLS:
-                    fill(b, k + AHEAD)
-
-        def statistics(b, pair):
-            for t in range(pair * PAIR, (pair + 1) * PAIR):
-                transpose_plane(b, t)
-                centred_squares(b, t)
-            scale_of(b, pair)
-
         for t in range(PACK):
             token_sums(0, t)
         means(0)
+        for t in range(PACK):
+            transpose_plane(0, t)
+            centred_squares(0, t)
+            if t % PAIR == PAIR - 1:
+                scale_of(0, t // PAIR)
         for pair in range(2):
-            statistics(0, pair)
-        shift_of(0)
+            shift_of(0, pair)
 
         pos_t = const.tile([P, PACK, TOKENS], BF16)
         for t in range(PACK):
@@ -245,7 +246,6 @@ def tile_attentionblock_pa_t_kernel(tc, x, pos_enc, gamma1, beta1, W_qkv, b_qkv,
             nc.vector.tensor_copy(out=pos_t[:, t, :], in_=pos_ps[:])
         for t in range(PACK):
             token_sums(1, t)
-        means(1)
 
         w_grp = const.tile([P, D_OUT, PACK], BF16, align_bytes=64)
         w_codes = const.tile([P, D_OUT], U32, align_bytes=64)
@@ -260,36 +260,39 @@ def tile_attentionblock_pa_t_kernel(tc, x, pos_enc, gamma1, beta1, W_qkv, b_qkv,
                     in_=w_grp[:, w_cols, :].rearrange("p n t -> p (n t)"),
                 )
 
-        for b in range(BATCH + 2):
-            for pair in range(2):
-                for t in range(pair * PAIR, (pair + 1) * PAIR):
-                    if b < BATCH:
-                        normalise_plane(b, t)
-                    if b + 1 < BATCH:
-                        transpose_plane(b + 1, t)
-                        centred_squares(b + 1, t)
-                    if b + 2 < BATCH:
-                        token_sums(b + 2, t)
-                if b + 1 < BATCH:
-                    scale_of(b + 1, pair)
+        for quarter in range(BATCH * QUARTERS + DRAIN_LAG):
+            b, q = divmod(quarter, QUARTERS)
+            if q == 0 and b + 1 < BATCH:
+                means(b + 1)
+            if b < BATCH:
+                normalise_plane(b, q)
+                swish(b, q)
             if b + 1 < BATCH:
-                shift_of(b + 1)
-            if b < BATCH:
-                swish(b)
-            if b >= 2:
-                finish(b - 2, 0)
-            if b == 1:
-                quantise_weights()
-            if 1 <= b <= BATCH:
-                for half in range(2):
-                    quantise(b - 1, half)
-            if b >= 2:
-                finish(b - 2, 1)
-            if 1 <= b <= BATCH:
-                for k in range(AHEAD):
-                    fill(b - 1, k)
-            if b < BATCH:
-                for half in range(2):
-                    regroup(b, half)
+                transpose_plane(b + 1, q)
+                centred_squares(b + 1, q)
             if b + 2 < BATCH:
-                means(b + 2)
+                token_sums(b + 2, q)
+            if 1 <= b <= BATCH:
+                regroup(b - 1, q)
+            if q == 1:
+                if b + 1 < BATCH:
+                    scale_of(b + 1, 0)
+                if 1 <= b < BATCH:
+                    shift_of(b, 1)
+            if q == 3:
+                if b + 1 < BATCH:
+                    scale_of(b + 1, 1)
+                    shift_of(b + 1, 0)
+            if quarter == QUARTERS - 1:
+                quantise_weights()
+            if q == 2 and 1 <= b <= BATCH:
+                quantise(b - 1, 0)
+                to_fill.extend([(b - 1, 0, i) for i in range(BANKS_PER_HALF)])
+            if q == 0 and 2 <= b <= BATCH + 1:
+                quantise(b - 2, 1)
+                to_fill.extend([(b - 2, 1, i) for i in range(BANKS_PER_HALF)])
+            fill_free_banks()
+            if quarter >= DRAIN_LAG:
+                for i in range(BANKS_PER_HALF // 2 + (quarter - DRAIN_LAG + 1) % 2):
+                    drain()
+                    fill_free_banks()

@@ -26,8 +26,9 @@ PAIR = PACK // 2
 WIDE = 512
 NARROW = D_OUT - WIDE
 BANKS_PER_HALF = 1 + HALF_TILES
+VECTOR_STATS = ((0, 0), (1, 1))
 DRAIN_LAG = 7
-SUM_COLS = 48
+SUM_COLS = 72
 AHEAD = 3
 STORE_TILES = 2
 EPS = 1e-5
@@ -53,7 +54,10 @@ def tile_attentionblock_pa_t_kernel(tc, x, pos_enc, gamma1, beta1, W_qkv, b_qkv,
             x_nat[b] = const.tile([P, TILES, D_IN], BF16, name="x%d" % b)
             nc.sync.dma_start(out=x_nat[b][:], in_=x[b, :, :].rearrange("(p j) d -> p j d", j=TILES))
 
-        load_x(0)
+        x_nat[0] = const.tile([P, TILES, D_IN], BF16, name="x0")
+        for half in range(2):
+            tiles = slice(half * HALF_TILES, (half + 1) * HALF_TILES)
+            nc.sync.dma_start(out=x_nat[0][:, tiles, :], in_=x[0, :, :].rearrange("(p j) d -> p j d", j=TILES)[:, tiles, :])
         nc.sync.dma_start(out=gamma[:], in_=gamma1[0, :, :].rearrange("a (p t) -> (a p) t", t=PACK))
         nc.sync.dma_start(out=beta[:], in_=beta1[0, :, :].rearrange("a (p t) -> (a p) t", t=PACK))
         pos_nat = const.tile([P, TILES, D_IN], BF16)
@@ -76,12 +80,14 @@ def tile_attentionblock_pa_t_kernel(tc, x, pos_enc, gamma1, beta1, W_qkv, b_qkv,
         nc.vector.memset(warm[:], 0.0)
         nc.scalar.activation(out=warm[:], in_=warm[:], func=ACT.Silu)
 
-        sums, neg_mean, sum_sq, var_eps, scale, shift = {}, {}, {}, {}, {}, {}
+        sums, mean_var, neg_mean, sum_sq, var_eps, scale, shift = {}, {}, {}, {}, {}, {}, {}
         x_t, h_pl, a_pl, a_grp, a_codes, a_scales = {}, {}, {}, {}, {}, {}
         prod, out_sb = {}, {}
 
         def token_sums(b, t):
-            if t == 0:
+            if (b, t // PAIR) in VECTOR_STATS:
+                return
+            if b not in sums:
                 sums[b] = psum.tile([P, PACK, SUM_COLS], F32, name="sums")
             for j in range(TILES):
                 nc.tensor.matmul(
@@ -94,7 +100,12 @@ def tile_attentionblock_pa_t_kernel(tc, x, pos_enc, gamma1, beta1, W_qkv, b_qkv,
 
         def means(b):
             neg_mean[b] = small.tile([P, PACK], F32, name="neg_mean")
-            nc.scalar.activation(out=neg_mean[b][:], in_=sums[b][:, :, 0], func=ACT.Copy, scale=-1.0 / TOKENS)
+            for pair in range(2):
+                if (b, pair) not in VECTOR_STATS:
+                    planes = slice(pair * PAIR, (pair + 1) * PAIR)
+                    nc.scalar.activation(
+                        out=neg_mean[b][:, planes], in_=sums[b][:, planes, 0], func=ACT.Copy, scale=-1.0 / TOKENS
+                    )
             sum_sq[b] = small.tile([P, PACK], F32, name="sum_sq")
             var_eps[b] = small.tile([P, PACK], F32, name="var_eps")
             scale[b] = small.tile([P, PACK], F32, name="scale")
@@ -116,9 +127,23 @@ def tile_attentionblock_pa_t_kernel(tc, x, pos_enc, gamma1, beta1, W_qkv, b_qkv,
                 accum_out=sum_sq[b][:, t : t + 1],
             )
 
+        def vector_stats(b, pair):
+            mean_var[b] = small.tile([P, PAIR, 2], F32, name="mean_var")
+            for t in range(pair * PAIR, (pair + 1) * PAIR):
+                parts = small.tile([P, 2, 6], F32, name="parts")
+                for half in range(2):
+                    nc.vector.bn_stats(out=parts[:, half, :], in_=x_t[b, t][:, half * HALF : (half + 1) * HALF])
+                nc.vector.bn_aggr(out=mean_var[b][:, t % PAIR, :], in_=parts[:].rearrange("p h s -> p (h s)"))
+
         def scale_of(b, pair):
             planes = slice(pair * PAIR, (pair + 1) * PAIR)
-            nc.scalar.activation(out=var_eps[b][:, planes], in_=sum_sq[b][:, planes], func=ACT.Copy, scale=1.0 / TOKENS, bias=EPS)
+            if (b, pair) in VECTOR_STATS:
+                nc.scalar.activation(out=var_eps[b][:, planes], in_=mean_var[b][:, :, 1], func=ACT.Copy, scale=1.0, bias=EPS)
+                nc.scalar.activation(out=neg_mean[b][:, planes], in_=mean_var[b][:, :, 0], func=ACT.Copy, scale=-1.0)
+            else:
+                nc.scalar.activation(
+                    out=var_eps[b][:, planes], in_=sum_sq[b][:, planes], func=ACT.Copy, scale=1.0 / TOKENS, bias=EPS
+                )
             rstd = small.tile([P, PAIR], F32, name="rstd")
             nc.gpsimd.tensor_tensor(out=rstd[:], in0=var_eps[b][:, planes], in1=minus_half[:], op=ALU.pow)
             nc.gpsimd.tensor_tensor(out=scale[b][:, planes], in0=rstd[:], in1=gamma[:, planes], op=ALU.mult)
@@ -227,22 +252,30 @@ def tile_attentionblock_pa_t_kernel(tc, x, pos_enc, gamma1, beta1, W_qkv, b_qkv,
                         out=out[b, :, :].rearrange("(p j) c -> p j c", j=TILES)[:, done, :], in_=out_sb[b][:, done, :]
                     )
 
-        for t in range(PACK):
-            token_sums(0, t)
-        means(0)
-        for t in range(PACK):
-            transpose_plane(0, t)
-            centred_squares(0, t)
-            if t % PAIR == PAIR - 1:
-                scale_of(0, t // PAIR)
-        for pair in range(2):
-            shift_of(0, pair)
-
         pos_t = const.tile([P, PACK, TOKENS], BF16)
-        for t in range(PACK):
+
+        def transpose_pos(t):
             pos_ps = psum.tile([P, TOKENS], BF16, name="pos_ps", tag="prod", bufs=AHEAD)
             for j in range(TILES):
                 nc.tensor.transpose(pos_ps[:, j * P : (j + 1) * P], pos_nat[:, j, t:D_IN:PACK], ident[:])
+            return pos_ps
+
+        for t in range(PAIR):
+            transpose_plane(0, t)
+        vector_stats(0, 0)
+        for t in range(PAIR, PACK):
+            token_sums(0, t)
+        means(0)
+        for t in range(PAIR, PACK):
+            transpose_plane(0, t)
+        scale_of(0, 0)
+        shift_of(0, 0)
+        for t in range(PAIR, PACK):
+            centred_squares(0, t)
+        scale_of(0, 1)
+        shift_of(0, 1)
+        for t in range(PACK):
+            pos_ps = transpose_pos(t)
             nc.vector.tensor_copy(out=pos_t[:, t, :], in_=pos_ps[:])
         for t in range(PACK):
             token_sums(1, t)
@@ -251,8 +284,11 @@ def tile_attentionblock_pa_t_kernel(tc, x, pos_enc, gamma1, beta1, W_qkv, b_qkv,
         w_codes = const.tile([P, D_OUT], U32, align_bytes=64)
         w_scales = const.tile([P, D_OUT], U8, align_bytes=64)
 
+        nc.gpsimd.tensor_scalar(
+            out=w_grp[:], in0=w_raw[:].rearrange("p t n -> p n t"), scalar1=1.0, scalar2=0.0, op0=ALU.mult, op1=ALU.add
+        )
+
         def quantise_weights():
-            nc.vector.tensor_copy(out=w_grp[:], in_=w_raw[:].rearrange("p t n -> p n t"))
             for w_cols in (slice(0, WIDE), slice(WIDE, D_OUT)):
                 nc.vector.quantize_mx(
                     out=w_codes[:, w_cols].bitcast(FP8X4),
@@ -269,7 +305,8 @@ def tile_attentionblock_pa_t_kernel(tc, x, pos_enc, gamma1, beta1, W_qkv, b_qkv,
                 swish(b, q)
             if b + 1 < BATCH:
                 transpose_plane(b + 1, q)
-                centred_squares(b + 1, q)
+                if (b + 1, q // PAIR) not in VECTOR_STATS:
+                    centred_squares(b + 1, q)
             if b + 2 < BATCH:
                 token_sums(b + 2, q)
             if 1 <= b <= BATCH:
@@ -280,10 +317,12 @@ def tile_attentionblock_pa_t_kernel(tc, x, pos_enc, gamma1, beta1, W_qkv, b_qkv,
                 if 1 <= b < BATCH:
                     shift_of(b, 1)
             if q == 3:
+                if (b + 1, 1) in VECTOR_STATS:
+                    vector_stats(b + 1, 1)
                 if b + 1 < BATCH:
                     scale_of(b + 1, 1)
                     shift_of(b + 1, 0)
-            if quarter == QUARTERS - 1:
+            if quarter == QUARTERS:
                 quantise_weights()
             if q == 2 and 1 <= b <= BATCH:
                 quantise(b - 1, 0)

@@ -26,9 +26,11 @@ PAIR = PACK // 2
 WIDE = 512
 NARROW = D_OUT - WIDE
 BANKS_PER_HALF = 1 + HALF_TILES
-VECTOR_STATS = ((0, 0), (1, 1))
+VECTOR_STATS = ((0, 0), (0, 1))
 DRAIN_LAG = 7
-SUM_COLS = 72
+SUM_COLS = 60
+LEAD = 16
+SQ_COLS = P + 1
 AHEAD = 3
 STORE_TILES = 2
 EPS = 1e-5
@@ -54,6 +56,10 @@ def tile_attentionblock_pa_t_kernel(tc, x, pos_enc, gamma1, beta1, W_qkv, b_qkv,
             x_nat[b] = const.tile([P, TILES, D_IN], BF16, name="x%d" % b)
             nc.sync.dma_start(out=x_nat[b][:], in_=x[b, :, :].rearrange("(p j) d -> p j d", j=TILES))
 
+        x_own = const.tile([P, TILES, LEAD + D_IN], BF16, align_bytes=64)
+        nc.gpsimd.memset(x_own[:, :, 0:LEAD], 1.0)
+        x_nat[1] = x_own[:, :, LEAD : LEAD + D_IN]
+
         x_nat[0] = const.tile([P, TILES, D_IN], BF16, name="x0")
         for half in range(2):
             tiles = slice(half * HALF_TILES, (half + 1) * HALF_TILES)
@@ -62,7 +68,7 @@ def tile_attentionblock_pa_t_kernel(tc, x, pos_enc, gamma1, beta1, W_qkv, b_qkv,
         nc.sync.dma_start(out=beta[:], in_=beta1[0, :, :].rearrange("a (p t) -> (a p) t", t=PACK))
         pos_nat = const.tile([P, TILES, D_IN], BF16)
         nc.sync.dma_start(out=pos_nat[:], in_=pos_enc[0, :, :].rearrange("(p j) d -> p j d", j=TILES))
-        load_x(1)
+        nc.sync.dma_start(out=x_nat[1], in_=x[1, :, :].rearrange("(p j) d -> p j d", j=TILES))
         w_raw = const.tile([P, PACK, D_OUT], BF16)
         nc.sync.dma_start(out=w_raw[:], in_=W_qkv.rearrange("(p t) n -> p t n", t=PACK))
         bias_bc = const.tile([P, D_OUT], BF16)
@@ -72,6 +78,8 @@ def tile_attentionblock_pa_t_kernel(tc, x, pos_enc, gamma1, beta1, W_qkv, b_qkv,
 
         ident = const.tile([P, P], BF16)
         masks.make_identity(nc, ident[:])
+        ident_f = const.tile([P, P], F32)
+        masks.make_identity(nc, ident_f[:])
         ones = const.tile([P, SUM_COLS], BF16)
         nc.vector.memset(ones[:], 1.0)
         minus_half = const.tile([P, PAIR], F32)
@@ -82,10 +90,22 @@ def tile_attentionblock_pa_t_kernel(tc, x, pos_enc, gamma1, beta1, W_qkv, b_qkv,
 
         sums, mean_var, neg_mean, sum_sq, var_eps, scale, shift = {}, {}, {}, {}, {}, {}, {}
         x_t, h_pl, a_pl, a_grp, a_codes, a_scales = {}, {}, {}, {}, {}, {}
-        prod, out_sb = {}, {}
+        prod, out_sb, own = {}, {}, {}
 
         def token_sums(b, t):
             if (b, t // PAIR) in VECTOR_STATS:
+                return
+            if b == 1:
+                if t % PAIR == 0:
+                    own[t // PAIR] = psum.tile([P, PAIR, SQ_COLS], F32, name="own", tag="prod", bufs=AHEAD)
+                for j in range(TILES):
+                    nc.tensor.matmul(
+                        out=own[t // PAIR][:, t % PAIR, :],
+                        lhsT=x_nat[b][:, j, t:D_IN:PACK],
+                        rhs=x_own[:, j, LEAD - PACK + t : LEAD + D_IN : PACK],
+                        start=(j == 0),
+                        stop=(j == TILES - 1),
+                    )
                 return
             if b not in sums:
                 sums[b] = psum.tile([P, PACK, SUM_COLS], F32, name="sums")
@@ -100,16 +120,37 @@ def tile_attentionblock_pa_t_kernel(tc, x, pos_enc, gamma1, beta1, W_qkv, b_qkv,
 
         def means(b):
             neg_mean[b] = small.tile([P, PACK], F32, name="neg_mean")
-            for pair in range(2):
-                if (b, pair) not in VECTOR_STATS:
-                    planes = slice(pair * PAIR, (pair + 1) * PAIR)
+            if b == 1:
+                for pair in range(2):
                     nc.scalar.activation(
-                        out=neg_mean[b][:, planes], in_=sums[b][:, planes, 0], func=ACT.Copy, scale=-1.0 / TOKENS
+                        out=neg_mean[b][:, pair * PAIR : (pair + 1) * PAIR],
+                        in_=own[pair][:, :, 0],
+                        func=ACT.Copy,
+                        scale=-1.0 / TOKENS,
                     )
+            if b > 1:
+                nc.scalar.activation(out=neg_mean[b][:], in_=sums[b][:, :, 0], func=ACT.Copy, scale=-1.0 / TOKENS)
             sum_sq[b] = small.tile([P, PACK], F32, name="sum_sq")
             var_eps[b] = small.tile([P, PACK], F32, name="var_eps")
             scale[b] = small.tile([P, PACK], F32, name="scale")
             shift[b] = small.tile([P, PACK], F32, name="shift")
+
+        def own_stats(b, mean_sq):
+            sq = small.tile([P, PACK], F32, name="sq")
+            for t in range(PACK):
+                unused_d = work.tile([P, P], F32, name="unused_d")
+                nc.vector.scalar_tensor_tensor(
+                    out=unused_d[:],
+                    in0=own[t // PAIR][:, t % PAIR, 1:SQ_COLS],
+                    scalar=1.0 / TOKENS,
+                    in1=ident_f[:],
+                    op0=ALU.mult,
+                    op1=ALU.mult,
+                    accum_out=sq[:, t : t + 1],
+                )
+            var = small.tile([P, PACK], F32, name="var")
+            nc.vector.tensor_tensor(out=var[:], in0=sq[:], in1=mean_sq[:], op=ALU.subtract)
+            nc.vector.tensor_scalar(out=var_eps[b][:], in0=var[:], scalar1=0.0, scalar2=EPS, op0=ALU.max, op1=ALU.add)
 
         def transpose_plane(b, t):
             x_t[b, t] = psum.tile([P, TOKENS], BF16, name="x_t", tag="x_t%d" % t)
@@ -128,19 +169,19 @@ def tile_attentionblock_pa_t_kernel(tc, x, pos_enc, gamma1, beta1, W_qkv, b_qkv,
             )
 
         def vector_stats(b, pair):
-            mean_var[b] = small.tile([P, PAIR, 2], F32, name="mean_var")
+            mean_var[b, pair] = small.tile([P, PAIR, 2], F32, name="mean_var")
             for t in range(pair * PAIR, (pair + 1) * PAIR):
                 parts = small.tile([P, 2, 6], F32, name="parts")
                 for half in range(2):
                     nc.vector.bn_stats(out=parts[:, half, :], in_=x_t[b, t][:, half * HALF : (half + 1) * HALF])
-                nc.vector.bn_aggr(out=mean_var[b][:, t % PAIR, :], in_=parts[:].rearrange("p h s -> p (h s)"))
+                nc.vector.bn_aggr(out=mean_var[b, pair][:, t % PAIR, :], in_=parts[:].rearrange("p h s -> p (h s)"))
 
         def scale_of(b, pair):
             planes = slice(pair * PAIR, (pair + 1) * PAIR)
             if (b, pair) in VECTOR_STATS:
-                nc.scalar.activation(out=var_eps[b][:, planes], in_=mean_var[b][:, :, 1], func=ACT.Copy, scale=1.0, bias=EPS)
-                nc.scalar.activation(out=neg_mean[b][:, planes], in_=mean_var[b][:, :, 0], func=ACT.Copy, scale=-1.0)
-            else:
+                nc.scalar.activation(out=var_eps[b][:, planes], in_=mean_var[b, pair][:, :, 1], func=ACT.Copy, scale=1.0, bias=EPS)
+                nc.scalar.activation(out=neg_mean[b][:, planes], in_=mean_var[b, pair][:, :, 0], func=ACT.Copy, scale=-1.0)
+            elif b != 1:
                 nc.scalar.activation(
                     out=var_eps[b][:, planes], in_=sum_sq[b][:, planes], func=ACT.Copy, scale=1.0 / TOKENS, bias=EPS
                 )
@@ -260,23 +301,19 @@ def tile_attentionblock_pa_t_kernel(tc, x, pos_enc, gamma1, beta1, W_qkv, b_qkv,
                 nc.tensor.transpose(pos_ps[:, j * P : (j + 1) * P], pos_nat[:, j, t:D_IN:PACK], ident[:])
             return pos_ps
 
-        for t in range(PAIR):
+        for t in range(PACK):
             transpose_plane(0, t)
-        vector_stats(0, 0)
-        for t in range(PAIR, PACK):
-            token_sums(0, t)
         means(0)
-        for t in range(PAIR, PACK):
-            transpose_plane(0, t)
+        vector_stats(0, 0)
         scale_of(0, 0)
         shift_of(0, 0)
-        for t in range(PAIR, PACK):
-            centred_squares(0, t)
-        scale_of(0, 1)
-        shift_of(0, 1)
+        vector_stats(0, 1)
         for t in range(PACK):
+            if t == PAIR:
+                scale_of(0, 1)
             pos_ps = transpose_pos(t)
-            nc.vector.tensor_copy(out=pos_t[:, t, :], in_=pos_ps[:])
+            nc.scalar.copy(out=pos_t[:, t, :], in_=pos_ps[:])
+        shift_of(0, 1)
         for t in range(PACK):
             token_sums(1, t)
 
@@ -296,42 +333,55 @@ def tile_attentionblock_pa_t_kernel(tc, x, pos_enc, gamma1, beta1, W_qkv, b_qkv,
                     in_=w_grp[:, w_cols, :].rearrange("p n t -> p (n t)"),
                 )
 
-        for quarter in range(BATCH * QUARTERS + DRAIN_LAG):
+        DL = 1
+        RG = lambda b, i: 4 * b + 4 + i if b else (3, 3, 4, 5)[i]
+        KQ = lambda b, h: 4 * b + 6 + 2 * h if b else (5, 7)[h]
+        DR = lambda k: 0 if k < 6 else 2 + k % 2
+        WQ = 4
+        for quarter in range(BATCH * QUARTERS + DRAIN_LAG + 3):
             b, q = divmod(quarter, QUARTERS)
-            if q == 0 and b + 1 < BATCH:
+            if q == 0 and 1 <= b and b + 1 < BATCH:
                 means(b + 1)
             if b < BATCH:
                 normalise_plane(b, q)
                 swish(b, q)
             if b + 1 < BATCH:
                 transpose_plane(b + 1, q)
-                if (b + 1, q // PAIR) not in VECTOR_STATS:
+                if b >= 1:
                     centred_squares(b + 1, q)
+            if quarter == 1:
+                means(1)
+                mean_sq = small.tile([P, PACK], F32, name="mean_sq")
+                nc.scalar.activation(out=mean_sq[:], in_=neg_mean[1][:], func=ACT.Square)
+            if quarter == 3:
+                own_stats(1, mean_sq)
+                scale_of(1, 0)
+                scale_of(1, 1)
+                shift_of(1, 0)
             if b + 2 < BATCH:
                 token_sums(b + 2, q)
-            if 1 <= b <= BATCH:
-                regroup(b - 1, q)
+            for rb in range(BATCH):
+                for piece in range(QUARTERS):
+                    if RG(rb, piece) == quarter:
+                        regroup(rb, piece)
             if q == 1:
-                if b + 1 < BATCH:
+                if b >= 1 and b + 1 < BATCH:
                     scale_of(b + 1, 0)
                 if 1 <= b < BATCH:
                     shift_of(b, 1)
             if q == 3:
-                if (b + 1, 1) in VECTOR_STATS:
-                    vector_stats(b + 1, 1)
-                if b + 1 < BATCH:
+                if 1 <= b and b + 1 < BATCH:
                     scale_of(b + 1, 1)
                     shift_of(b + 1, 0)
-            if quarter == QUARTERS:
+            if quarter == WQ:
                 quantise_weights()
-            if q == 2 and 1 <= b <= BATCH:
-                quantise(b - 1, 0)
-                to_fill.extend([(b - 1, 0, i) for i in range(BANKS_PER_HALF)])
-            if q == 0 and 2 <= b <= BATCH + 1:
-                quantise(b - 2, 1)
-                to_fill.extend([(b - 2, 1, i) for i in range(BANKS_PER_HALF)])
+            for rb in range(BATCH):
+                for half in range(2):
+                    if KQ(rb, half) == quarter:
+                        quantise(rb, half)
+                        to_fill.extend([(rb, half, i) for i in range(BANKS_PER_HALF)])
             fill_free_banks()
-            if quarter >= DRAIN_LAG:
-                for i in range(BANKS_PER_HALF // 2 + (quarter - DRAIN_LAG + 1) % 2):
+            for i in range(DR(quarter)):
+                if to_drain and KQ(*to_drain[0][:2]) + DL <= quarter:
                     drain()
                     fill_free_banks()

@@ -64,16 +64,19 @@ def tile_attentionblock_pa_t_kernel(tc, x, pos_enc, gamma1, beta1, W_qkv, b_qkv,
         for half in range(2):
             tiles = slice(half * HALF_TILES, (half + 1) * HALF_TILES)
             nc.sync.dma_start(out=x_nat[0][:, tiles, :], in_=x[0, :, :].rearrange("(p j) d -> p j d", j=TILES)[:, tiles, :])
-        nc.sync.dma_start(out=gamma[:], in_=gamma1[0, :, :].rearrange("a (p t) -> (a p) t", t=PACK))
-        nc.sync.dma_start(out=beta[:], in_=beta1[0, :, :].rearrange("a (p t) -> (a p) t", t=PACK))
+        nc.scalar.dma_start(out=gamma[:], in_=gamma1[0, :, :].rearrange("a (p t) -> (a p) t", t=PACK))
+        nc.scalar.dma_start(out=beta[:], in_=beta1[0, :, :].rearrange("a (p t) -> (a p) t", t=PACK))
         pos_nat = const.tile([P, TILES, D_IN], BF16)
         nc.sync.dma_start(out=pos_nat[:], in_=pos_enc[0, :, :].rearrange("(p j) d -> p j d", j=TILES))
         nc.sync.dma_start(out=x_nat[1], in_=x[1, :, :].rearrange("(p j) d -> p j d", j=TILES))
+        load_x(2)
         w_raw = const.tile([P, PACK, D_OUT], BF16)
         nc.sync.dma_start(out=w_raw[:], in_=W_qkv.rearrange("(p t) n -> p t n", t=PACK))
+        for b in range(3, 5):
+            load_x(b)
         bias_bc = const.tile([P, D_OUT], BF16)
         nc.sync.dma_start(out=bias_bc[:], in_=b_qkv.partition_broadcast(P))
-        for b in range(2, BATCH):
+        for b in range(5, BATCH):
             load_x(b)
 
         ident = const.tile([P, P], BF16)

@@ -20,9 +20,10 @@ D_OUT = 640
 TILES = TOKENS // P
 HALF_TILES = TILES // 2
 HALF = TOKENS // 2
+PAIR = PACK // 2
+WORDS = D_IN // PAIR
 QUARTERS = PACK
 PIECE = TOKENS // QUARTERS
-PAIR = PACK // 2
 WIDE = 512
 NARROW = D_OUT - WIDE
 BANKS_PER_HALF = 1 + HALF_TILES
@@ -93,7 +94,7 @@ def tile_attentionblock_pa_t_kernel(tc, x, pos_enc, gamma1, beta1, W_qkv, b_qkv,
 
         sums, mean_var, neg_mean, sum_sq, var_eps, scale, shift = {}, {}, {}, {}, {}, {}, {}
         x_t, h_pl, a_pl, a_grp, a_codes, a_scales = {}, {}, {}, {}, {}, {}
-        prod, out_sb, own = {}, {}, {}
+        prod, out_sb, own, mean_sq = {}, {}, {}, {}
 
         def token_sums(b, t):
             if (b, t // PAIR) in VECTOR_STATS:
@@ -123,14 +124,6 @@ def tile_attentionblock_pa_t_kernel(tc, x, pos_enc, gamma1, beta1, W_qkv, b_qkv,
 
         def means(b):
             neg_mean[b] = small.tile([P, PACK], F32, name="neg_mean")
-            if b == 1:
-                for pair in range(2):
-                    nc.scalar.activation(
-                        out=neg_mean[b][:, pair * PAIR : (pair + 1) * PAIR],
-                        in_=own[pair][:, :, 0],
-                        func=ACT.Copy,
-                        scale=-1.0 / TOKENS,
-                    )
             if b > 1:
                 nc.scalar.activation(out=neg_mean[b][:], in_=sums[b][:, :, 0], func=ACT.Copy, scale=-1.0 / TOKENS)
             sum_sq[b] = small.tile([P, PACK], F32, name="sum_sq")
@@ -138,22 +131,30 @@ def tile_attentionblock_pa_t_kernel(tc, x, pos_enc, gamma1, beta1, W_qkv, b_qkv,
             scale[b] = small.tile([P, PACK], F32, name="scale")
             shift[b] = small.tile([P, PACK], F32, name="shift")
 
-        def own_stats(b, mean_sq):
-            sq = small.tile([P, PACK], F32, name="sq")
-            for t in range(PACK):
+        def own_means(b, pair):
+            planes = slice(pair * PAIR, (pair + 1) * PAIR)
+            nc.scalar.activation(out=neg_mean[b][:, planes], in_=own[pair][:, :, 0], func=ACT.Copy, scale=-1.0 / TOKENS)
+            mean_sq[pair] = small.tile([P, PAIR], F32, name="mean_sq")
+            nc.scalar.activation(out=mean_sq[pair][:], in_=neg_mean[b][:, planes], func=ACT.Square)
+
+        def own_stats(b, pair):
+            planes = slice(pair * PAIR, (pair + 1) * PAIR)
+            sq = small.tile([P, PAIR], F32, name="sq")
+            for t in range(PAIR):
                 unused_d = work.tile([P, P], F32, name="unused_d")
                 nc.vector.scalar_tensor_tensor(
                     out=unused_d[:],
-                    in0=own[t // PAIR][:, t % PAIR, 1:SQ_COLS],
+                    in0=own[pair][:, t, 1:SQ_COLS],
                     scalar=1.0 / TOKENS,
                     in1=ident_f[:],
                     op0=ALU.mult,
                     op1=ALU.mult,
                     accum_out=sq[:, t : t + 1],
                 )
-            var = small.tile([P, PACK], F32, name="var")
-            nc.vector.tensor_tensor(out=var[:], in0=sq[:], in1=mean_sq[:], op=ALU.subtract)
-            nc.vector.tensor_scalar(out=var_eps[b][:], in0=var[:], scalar1=0.0, scalar2=EPS, op0=ALU.max, op1=ALU.add)
+            var = small.tile([P, PAIR], F32, name="var")
+            nc.vector.tensor_tensor(out=var[:], in0=sq[:], in1=mean_sq[pair][:], op=ALU.subtract)
+            nc.vector.tensor_scalar(out=var_eps[b][:, planes], in0=var[:], scalar1=0.0, scalar2=EPS, op0=ALU.max, op1=ALU.add)
+            scale_of(b, pair)
 
         def transpose_plane(b, t):
             x_t[b, t] = psum.tile([P, TOKENS], BF16, name="x_t", tag="x_t%d" % t)
@@ -209,7 +210,7 @@ def tile_attentionblock_pa_t_kernel(tc, x, pos_enc, gamma1, beta1, W_qkv, b_qkv,
                 out=h_pl[b][:, t, :],
                 in0=x_t[b, t][:],
                 scalar=scale[b][:, t : t + 1],
-                in1=pos_t[:, t, :],
+                in1=pos_t[:, t // PAIR, :, t % PAIR],
                 op0=ALU.mult,
                 op1=ALU.add,
             )
@@ -296,26 +297,30 @@ def tile_attentionblock_pa_t_kernel(tc, x, pos_enc, gamma1, beta1, W_qkv, b_qkv,
                         out=out[b, :, :].rearrange("(p j) c -> p j c", j=TILES)[:, done, :], in_=out_sb[b][:, done, :]
                     )
 
-        pos_t = const.tile([P, PACK, TOKENS], BF16)
+        pos_t = const.tile([P, PAIR, TOKENS, PAIR], BF16)
+        pos_words = pos_t[:].rearrange("p u w e -> p (u w e)").bitcast(F32)
+        nat_words = pos_nat[:].rearrange("p j d -> p (j d)").bitcast(F32)
 
-        def transpose_pos(t):
-            pos_ps = psum.tile([P, TOKENS], BF16, name="pos_ps", tag="prod", bufs=AHEAD)
-            for j in range(TILES):
-                nc.tensor.transpose(pos_ps[:, j * P : (j + 1) * P], pos_nat[:, j, t:D_IN:PACK], ident[:])
-            return pos_ps
+        def place_pos(k):
+            u, half = divmod(k, 2)
+            pos_ps = psum.tile([P, HALF], F32, name="pos_ps", tag="prod", bufs=AHEAD)
+            for n in range(HALF_TILES):
+                first = (half * HALF_TILES + n) * WORDS
+                nc.tensor.transpose(pos_ps[:, n * P : (n + 1) * P], nat_words[:, first + u : first + WORDS : PAIR], ident_f[:])
+            nc.scalar.copy(out=pos_words[:, k * HALF : (k + 1) * HALF], in_=pos_ps[:])
 
         for t in range(PACK):
             transpose_plane(0, t)
         means(0)
         vector_stats(0, 0)
-        scale_of(0, 0)
-        shift_of(0, 0)
         vector_stats(0, 1)
-        for t in range(PACK):
-            if t == PAIR:
-                scale_of(0, 1)
-            pos_ps = transpose_pos(t)
-            nc.scalar.copy(out=pos_t[:, t, :], in_=pos_ps[:])
+        scale_of(0, 0)
+        place_pos(0)
+        place_pos(1)
+        shift_of(0, 0)
+        place_pos(2)
+        place_pos(3)
+        scale_of(0, 1)
         shift_of(0, 1)
         for t in range(PACK):
             token_sums(1, t)
@@ -352,14 +357,16 @@ def tile_attentionblock_pa_t_kernel(tc, x, pos_enc, gamma1, beta1, W_qkv, b_qkv,
                 transpose_plane(b + 1, q)
                 if b >= 1:
                     centred_squares(b + 1, q)
-            if quarter == 1:
+            if quarter == 0:
                 means(1)
-                mean_sq = small.tile([P, PACK], F32, name="mean_sq")
-                nc.scalar.activation(out=mean_sq[:], in_=neg_mean[1][:], func=ACT.Square)
+            if quarter == 1:
+                own_means(1, 0)
+            if quarter == 2:
+                own_means(1, 1)
             if quarter == 3:
-                own_stats(1, mean_sq)
-                scale_of(1, 0)
-                scale_of(1, 1)
+                own_stats(1, 0)
+                own_stats(1, 1)
+                quantise_weights()
                 shift_of(1, 0)
             if b + 2 < BATCH:
                 token_sums(b + 2, q)
@@ -376,8 +383,6 @@ def tile_attentionblock_pa_t_kernel(tc, x, pos_enc, gamma1, beta1, W_qkv, b_qkv,
                 if 1 <= b and b + 1 < BATCH:
                     scale_of(b + 1, 1)
                     shift_of(b + 1, 0)
-            if quarter == WQ:
-                quantise_weights()
             for rb in range(BATCH):
                 for half in range(2):
                     if KQ(rb, half) == quarter:

@@ -223,11 +223,15 @@ def tile_attentionblock_pa_t_kernel(tc, x, pos_enc, gamma1, beta1, W_qkv, b_qkv,
             )
 
         def regroup(b, piece):
-            if piece == 0:
-                a_grp[b] = work.tile([P, TOKENS, PACK], BF16, name="a_grp", align_bytes=64)
+            half, part = divmod(piece, 2)
+            if part == 0:
+                a_grp[b, half] = work.tile([P, HALF, PACK], BF16, name="a_grp", align_bytes=64, bufs=1)
             cols = slice(piece * PIECE, (piece + 1) * PIECE)
+            if b == BATCH - 1 and piece % 2 == 1:
+                nc.scalar.copy(out=a_grp[b, half][:, part * PIECE : (part + 1) * PIECE, :], in_=a_pl[b][:, :, cols].rearrange("p t w -> p w t"))
+                return
             nc.gpsimd.tensor_scalar(
-                out=a_grp[b][:, cols, :],
+                out=a_grp[b, half][:, part * PIECE : (part + 1) * PIECE, :],
                 in0=a_pl[b][:, :, cols].rearrange("p t w -> p w t"),
                 scalar1=1.0,
                 scalar2=0.0,
@@ -243,7 +247,7 @@ def tile_attentionblock_pa_t_kernel(tc, x, pos_enc, gamma1, beta1, W_qkv, b_qkv,
             nc.vector.quantize_mx(
                 out=a_codes[b][:, cols].bitcast(FP8X4),
                 scales=a_scales[b][:, cols],
-                in_=a_grp[b][:, cols, :].rearrange("p w t -> p (w t)"),
+                in_=a_grp[b, half][:].rearrange("p w t -> p (w t)"),
             )
 
         def multiply(b, j, acc, w_cols):
@@ -291,8 +295,9 @@ def tile_attentionblock_pa_t_kernel(tc, x, pos_enc, gamma1, beta1, W_qkv, b_qkv,
                 nc.vector.tensor_tensor(
                     out=out_sb[b][:, j, 0:WIDE], in0=prod[b, half, i][:], in1=bias_bc[:, 0:WIDE], op=ALU.add
                 )
-                if j % STORE_TILES == STORE_TILES - 1:
-                    done = slice(j + 1 - STORE_TILES, j + 1)
+                step = STORE_TILES if (b, j // STORE_TILES) != (BATCH - 1, TILES // STORE_TILES - 1) else 1
+                if j % step == step - 1:
+                    done = slice(j + 1 - step, j + 1)
                     nc.sync.dma_start(
                         out=out[b, :, :].rearrange("(p j) c -> p j c", j=TILES)[:, done, :], in_=out_sb[b][:, done, :]
                     )
@@ -342,7 +347,7 @@ def tile_attentionblock_pa_t_kernel(tc, x, pos_enc, gamma1, beta1, W_qkv, b_qkv,
                 )
 
         DL = 1
-        RG = lambda b, i: 4 * b + 4 + i if b else (3, 3, 4, 5)[i]
+        RG = lambda b, i: 4 * b + 4 + i if b else (3, 3, 5, 5)[i]
         KQ = lambda b, h: 4 * b + 6 + 2 * h if b else (5, 7)[h]
         DR = lambda k: 0 if k < 6 else 2 + k % 2
         WQ = 4
@@ -371,6 +376,11 @@ def tile_attentionblock_pa_t_kernel(tc, x, pos_enc, gamma1, beta1, W_qkv, b_qkv,
             if b + 2 < BATCH:
                 token_sums(b + 2, q)
             for rb in range(BATCH):
+                for half in range(2):
+                    if KQ(rb, half) == quarter:
+                        quantise(rb, half)
+                        to_fill.extend([(rb, half, i) for i in range(BANKS_PER_HALF)])
+            for rb in range(BATCH):
                 for piece in range(QUARTERS):
                     if RG(rb, piece) == quarter:
                         regroup(rb, piece)
@@ -383,11 +393,6 @@ def tile_attentionblock_pa_t_kernel(tc, x, pos_enc, gamma1, beta1, W_qkv, b_qkv,
                 if 1 <= b and b + 1 < BATCH:
                     scale_of(b + 1, 1)
                     shift_of(b + 1, 0)
-            for rb in range(BATCH):
-                for half in range(2):
-                    if KQ(rb, half) == quarter:
-                        quantise(rb, half)
-                        to_fill.extend([(rb, half, i) for i in range(BANKS_PER_HALF)])
             fill_free_banks()
             for i in range(DR(quarter)):
                 if to_drain and KQ(*to_drain[0][:2]) + DL <= quarter:

@@ -13,30 +13,41 @@ ALU = mybir.AluOpType
 
 P = 128
 PACK = 4
+PAIR = PACK // 2
 BATCH = 8
 TOKENS = 1024
 D_IN = P * PACK
 D_OUT = 640
 TILES = TOKENS // P
-HALF_TILES = TILES // 2
 HALF = TOKENS // 2
-PAIR = PACK // 2
-WORDS = D_IN // PAIR
+HALF_TILES = TILES // 2
 QUARTERS = PACK
-PIECE = TOKENS // QUARTERS
+WORDS = D_IN // PAIR
 WIDE = 512
 NARROW = D_OUT - WIDE
-BANKS_PER_HALF = 1 + HALF_TILES
-VECTOR_STATS = ((0, 0), (0, 1))
-DRAIN_LAG = 7
+BANKS = 3
+FIRST_DRAIN = 6
+LAST = BATCH - 1
 SUM_COLS = 60
 LEAD = 16
-SQ_COLS = P + 1
-AHEAD = 3
+OWN_COLS = 1 + P
+BIAS_ROUND = 3
 STORE_TILES = 2
 EPS = 1e-5
 
 FLOPS = 2 * BATCH * TOKENS * D_IN * D_OUT
+
+
+def regroup_at(b, half):
+    return QUARTERS * (b + 1) + 2 * half - (b == 0)
+
+
+def quantise_at(b, half):
+    return regroup_at(b, half) + 2
+
+
+def is_turned(b, half):
+    return (LAST - 2, 0) <= (b, half) < (LAST, 1)
 
 
 def tile_attentionblock_pa_t_kernel(tc, x, pos_enc, gamma1, beta1, W_qkv, b_qkv, out):
@@ -48,40 +59,40 @@ def tile_attentionblock_pa_t_kernel(tc, x, pos_enc, gamma1, beta1, W_qkv, b_qkv,
         psum = ctx.enter_context(tc.psum_pool(name="psum", bufs=1))
         ctx.enter_context(tc.manual_schedule())
 
-        gamma = const.tile([P, PACK], BF16)
-        beta = const.tile([P, PACK], BF16)
+        def natural(dram):
+            return dram.rearrange("(p j) d -> p j d", j=TILES)
 
-        x_nat = {}
-
-        def load_x(b):
-            x_nat[b] = const.tile([P, TILES, D_IN], BF16, name="x%d" % b)
-            nc.sync.dma_start(out=x_nat[b][:], in_=x[b, :, :].rearrange("(p j) d -> p j d", j=TILES))
-
-        x_own = const.tile([P, TILES, LEAD + D_IN], BF16, align_bytes=64)
-        nc.gpsimd.memset(x_own[:, :, 0:LEAD], 1.0)
-        x_nat[1] = x_own[:, :, LEAD : LEAD + D_IN]
-
-        x_nat[0] = const.tile([P, TILES, D_IN], BF16, name="x0")
+        x_nat = {0: const.tile([P, TILES, D_IN], BF16, name="x0")}
         for half in range(2):
             tiles = slice(half * HALF_TILES, (half + 1) * HALF_TILES)
-            nc.sync.dma_start(out=x_nat[0][:, tiles, :], in_=x[0, :, :].rearrange("(p j) d -> p j d", j=TILES)[:, tiles, :])
+            nc.sync.dma_start(out=x_nat[0][:, tiles, :], in_=natural(x[0, :, :])[:, tiles, :])
+        gamma = const.tile([P, PACK], BF16)
+        beta = const.tile([P, PACK], BF16)
         nc.scalar.dma_start(out=gamma[:], in_=gamma1[0, :, :].rearrange("a (p t) -> (a p) t", t=PACK))
         nc.scalar.dma_start(out=beta[:], in_=beta1[0, :, :].rearrange("a (p t) -> (a p) t", t=PACK))
         pos_nat = const.tile([P, TILES, D_IN], BF16)
-        nc.sync.dma_start(out=pos_nat[:], in_=pos_enc[0, :, :].rearrange("(p j) d -> p j d", j=TILES))
-        nc.sync.dma_start(out=x_nat[1], in_=x[1, :, :].rearrange("(p j) d -> p j d", j=TILES))
-        load_x(2)
+        nc.sync.dma_start(out=pos_nat[:], in_=natural(pos_enc[0, :, :]))
+        x_own = const.tile([P, TILES, LEAD + D_IN], BF16, align_bytes=64)
+        nc.gpsimd.memset(x_own[:, :, 0:LEAD], 1.0)
+        x_nat[1] = x_own[:, :, LEAD : LEAD + D_IN]
+        nc.sync.dma_start(out=x_nat[1], in_=natural(x[1, :, :]))
         w_raw = const.tile([P, PACK, D_OUT], BF16)
-        nc.sync.dma_start(out=w_raw[:], in_=W_qkv.rearrange("(p t) n -> p t n", t=PACK))
-        for b in range(3, 5):
-            load_x(b)
         bias_bc = const.tile([P, D_OUT], BF16)
+
+        def load_x(b):
+            x_nat[b] = const.tile([P, TILES, D_IN], BF16, name="x%d" % b)
+            nc.sync.dma_start(out=x_nat[b][:], in_=natural(x[b, :, :]))
+
+        nc.sync.dma_start(out=w_raw[:], in_=W_qkv.rearrange("(p t) n -> p t n", t=PACK))
+        for b in range(2, 5):
+            load_x(b)
         nc.sync.dma_start(out=bias_bc[:], in_=b_qkv.partition_broadcast(P))
         for b in range(5, BATCH):
             load_x(b)
 
         ident = const.tile([P, P], BF16)
         masks.make_identity(nc, ident[:])
+        bias_col = const.tile([P, 1], F32)
         ident_f = const.tile([P, P], F32)
         masks.make_identity(nc, ident_f[:])
         ones = const.tile([P, SUM_COLS], BF16)
@@ -92,27 +103,79 @@ def tile_attentionblock_pa_t_kernel(tc, x, pos_enc, gamma1, beta1, W_qkv, b_qkv,
         nc.vector.memset(warm[:], 0.0)
         nc.scalar.activation(out=warm[:], in_=warm[:], func=ACT.Silu)
 
-        sums, mean_var, neg_mean, sum_sq, var_eps, scale, shift = {}, {}, {}, {}, {}, {}, {}
-        x_t, h_pl, a_pl, a_grp, a_codes, a_scales = {}, {}, {}, {}, {}, {}
-        prod, out_sb, own, mean_sq = {}, {}, {}, {}
+        x_t, sums, own, mean_var, mean_sq = {}, {}, {}, {}, {}
+        neg_mean, sum_sq, var_eps, scale, shift = {}, {}, {}, {}, {}
+
+        def planes_of(pair):
+            return slice(pair * PAIR, (pair + 1) * PAIR)
+
+        def start_stats(b):
+            neg_mean[b] = small.tile([P, PACK], F32, name="neg_mean")
+            sum_sq[b] = small.tile([P, PACK], F32, name="sum_sq")
+            var_eps[b] = small.tile([P, PACK], F32, name="var_eps")
+            scale[b] = small.tile([P, PACK], F32, name="scale")
+            shift[b] = small.tile([P, PACK], F32, name="shift")
+
+        def transpose_plane(b, t):
+            x_t[b, t] = psum.tile([P, TOKENS], BF16, name="x_t", tag="x_t%d" % t)
+            for j in range(TILES):
+                nc.tensor.transpose(x_t[b, t][:, j * P : (j + 1) * P], x_nat[b][:, j, t:D_IN:PACK], ident[:])
+
+        def vector_stats(pair):
+            mean_var[pair] = small.tile([P, PAIR, 2], F32, name="mean_var")
+            for t in range(PAIR):
+                parts = small.tile([P, 2, 6], F32, name="parts")
+                for half in range(2):
+                    nc.vector.bn_stats(
+                        out=parts[:, half, :], in_=x_t[0, pair * PAIR + t][:, half * HALF : (half + 1) * HALF]
+                    )
+                nc.vector.bn_aggr(out=mean_var[pair][:, t, :], in_=parts[:].rearrange("p h s -> p (h s)"))
+
+        def own_products(t):
+            if t % PAIR == 0:
+                own[t // PAIR] = psum.tile([P, PAIR, OWN_COLS], F32, name="own", tag="prod", bufs=BANKS)
+            for j in range(TILES):
+                nc.tensor.matmul(
+                    out=own[t // PAIR][:, t % PAIR, :],
+                    lhsT=x_nat[1][:, j, t:D_IN:PACK],
+                    rhs=x_own[:, j, LEAD - PACK + t : LEAD + D_IN : PACK],
+                    start=(j == 0),
+                    stop=(j == TILES - 1),
+                )
+
+        def own_means(pair):
+            nc.scalar.activation(
+                out=neg_mean[1][:, planes_of(pair)], in_=own[pair][:, :, 0], func=ACT.Copy, scale=-1.0 / TOKENS
+            )
+            mean_sq[pair] = small.tile([P, PAIR], F32, name="mean_sq")
+            nc.scalar.activation(out=mean_sq[pair][:], in_=neg_mean[1][:, planes_of(pair)], func=ACT.Square)
+
+        def own_variances(pair):
+            squares = small.tile([P, PAIR], F32, name="squares")
+            for t in range(PAIR):
+                unused = work.tile([P, P], F32, name="unused_products")
+                nc.vector.scalar_tensor_tensor(
+                    out=unused[:],
+                    in0=own[pair][:, t, 1:OWN_COLS],
+                    scalar=1.0 / TOKENS,
+                    in1=ident_f[:],
+                    op0=ALU.mult,
+                    op1=ALU.mult,
+                    accum_out=squares[:, t : t + 1],
+                )
+            var = small.tile([P, PAIR], F32, name="var")
+            nc.vector.tensor_tensor(out=var[:], in0=squares[:], in1=mean_sq[pair][:], op=ALU.subtract)
+            nc.vector.tensor_scalar(
+                out=var_eps[1][:, planes_of(pair)], in0=var[:], scalar1=0.0, scalar2=EPS, op0=ALU.max, op1=ALU.add
+            )
 
         def token_sums(b, t):
-            if (b, t // PAIR) in VECTOR_STATS:
-                return
-            if b == 1:
-                if t % PAIR == 0:
-                    own[t // PAIR] = psum.tile([P, PAIR, SQ_COLS], F32, name="own", tag="prod", bufs=AHEAD)
-                for j in range(TILES):
+            if t == 0:
+                sums[b] = psum.tile([P, PACK + 1, SUM_COLS], F32, name="sums")
+                if b == BIAS_ROUND + 1:
                     nc.tensor.matmul(
-                        out=own[t // PAIR][:, t % PAIR, :],
-                        lhsT=x_nat[b][:, j, t:D_IN:PACK],
-                        rhs=x_own[:, j, LEAD - PACK + t : LEAD + D_IN : PACK],
-                        start=(j == 0),
-                        stop=(j == TILES - 1),
+                        out=sums[b][:, PACK, 0:2], lhsT=bias_bc[:, WIDE:D_OUT], rhs=ident[:, 0:2], start=True, stop=True
                     )
-                return
-            if b not in sums:
-                sums[b] = psum.tile([P, PACK, SUM_COLS], F32, name="sums")
             for j in range(TILES):
                 nc.tensor.matmul(
                     out=sums[b][:, t, :],
@@ -123,43 +186,8 @@ def tile_attentionblock_pa_t_kernel(tc, x, pos_enc, gamma1, beta1, W_qkv, b_qkv,
                 )
 
         def means(b):
-            neg_mean[b] = small.tile([P, PACK], F32, name="neg_mean")
-            if b > 1:
-                nc.scalar.activation(out=neg_mean[b][:], in_=sums[b][:, :, 0], func=ACT.Copy, scale=-1.0 / TOKENS)
-            sum_sq[b] = small.tile([P, PACK], F32, name="sum_sq")
-            var_eps[b] = small.tile([P, PACK], F32, name="var_eps")
-            scale[b] = small.tile([P, PACK], F32, name="scale")
-            shift[b] = small.tile([P, PACK], F32, name="shift")
-
-        def own_means(b, pair):
-            planes = slice(pair * PAIR, (pair + 1) * PAIR)
-            nc.scalar.activation(out=neg_mean[b][:, planes], in_=own[pair][:, :, 0], func=ACT.Copy, scale=-1.0 / TOKENS)
-            mean_sq[pair] = small.tile([P, PAIR], F32, name="mean_sq")
-            nc.scalar.activation(out=mean_sq[pair][:], in_=neg_mean[b][:, planes], func=ACT.Square)
-
-        def own_stats(b, pair):
-            planes = slice(pair * PAIR, (pair + 1) * PAIR)
-            sq = small.tile([P, PAIR], F32, name="sq")
-            for t in range(PAIR):
-                unused_d = work.tile([P, P], F32, name="unused_d")
-                nc.vector.scalar_tensor_tensor(
-                    out=unused_d[:],
-                    in0=own[pair][:, t, 1:SQ_COLS],
-                    scalar=1.0 / TOKENS,
-                    in1=ident_f[:],
-                    op0=ALU.mult,
-                    op1=ALU.mult,
-                    accum_out=sq[:, t : t + 1],
-                )
-            var = small.tile([P, PAIR], F32, name="var")
-            nc.vector.tensor_tensor(out=var[:], in0=sq[:], in1=mean_sq[pair][:], op=ALU.subtract)
-            nc.vector.tensor_scalar(out=var_eps[b][:, planes], in0=var[:], scalar1=0.0, scalar2=EPS, op0=ALU.max, op1=ALU.add)
-            scale_of(b, pair)
-
-        def transpose_plane(b, t):
-            x_t[b, t] = psum.tile([P, TOKENS], BF16, name="x_t", tag="x_t%d" % t)
-            for j in range(TILES):
-                nc.tensor.transpose(x_t[b, t][:, j * P : (j + 1) * P], x_nat[b][:, j, t:D_IN:PACK], ident[:])
+            start_stats(b)
+            nc.scalar.activation(out=neg_mean[b][:], in_=sums[b][:, 0:PACK, 0], func=ACT.Copy, scale=-1.0 / TOKENS)
 
         def centred_squares(b, t):
             unused = work.tile([P, TOKENS], BF16, name="unused")
@@ -172,20 +200,14 @@ def tile_attentionblock_pa_t_kernel(tc, x, pos_enc, gamma1, beta1, W_qkv, b_qkv,
                 accum_out=sum_sq[b][:, t : t + 1],
             )
 
-        def vector_stats(b, pair):
-            mean_var[b, pair] = small.tile([P, PAIR, 2], F32, name="mean_var")
-            for t in range(pair * PAIR, (pair + 1) * PAIR):
-                parts = small.tile([P, 2, 6], F32, name="parts")
-                for half in range(2):
-                    nc.vector.bn_stats(out=parts[:, half, :], in_=x_t[b, t][:, half * HALF : (half + 1) * HALF])
-                nc.vector.bn_aggr(out=mean_var[b, pair][:, t % PAIR, :], in_=parts[:].rearrange("p h s -> p (h s)"))
-
         def scale_of(b, pair):
-            planes = slice(pair * PAIR, (pair + 1) * PAIR)
-            if (b, pair) in VECTOR_STATS:
-                nc.scalar.activation(out=var_eps[b][:, planes], in_=mean_var[b, pair][:, :, 1], func=ACT.Copy, scale=1.0, bias=EPS)
-                nc.scalar.activation(out=neg_mean[b][:, planes], in_=mean_var[b, pair][:, :, 0], func=ACT.Copy, scale=-1.0)
-            elif b != 1:
+            planes = planes_of(pair)
+            if b == 0:
+                nc.scalar.activation(
+                    out=var_eps[b][:, planes], in_=mean_var[pair][:, :, 1], func=ACT.Copy, scale=1.0, bias=EPS
+                )
+                nc.scalar.activation(out=neg_mean[b][:, planes], in_=mean_var[pair][:, :, 0], func=ACT.Copy, scale=-1.0)
+            if b >= 2:
                 nc.scalar.activation(
                     out=var_eps[b][:, planes], in_=sum_sq[b][:, planes], func=ACT.Copy, scale=1.0 / TOKENS, bias=EPS
                 )
@@ -202,6 +224,21 @@ def tile_attentionblock_pa_t_kernel(tc, x, pos_enc, gamma1, beta1, W_qkv, b_qkv,
                     scale=neg_mean[b][:, t : t + 1],
                     bias=beta[:, t : t + 1],
                 )
+
+        h_pl, a_pl, a_grp, a_codes, a_scales = {}, {}, {}, {}, {}
+        pos_t = const.tile([P, PAIR, TOKENS, PAIR], BF16)
+        pos_words = pos_t[:].rearrange("p u w e -> p (u w e)").bitcast(F32)
+        nat_words = pos_nat[:].rearrange("p j d -> p (j d)").bitcast(F32)
+
+        def place_pos(u, half):
+            pos_ps = psum.tile([P, HALF], F32, name="pos_ps", tag="prod", bufs=BANKS)
+            for n in range(HALF_TILES):
+                first = (half * HALF_TILES + n) * WORDS
+                nc.tensor.transpose(
+                    pos_ps[:, n * P : (n + 1) * P], nat_words[:, first + u : first + WORDS : PAIR], ident_f[:]
+                )
+            start = u * TOKENS + half * HALF
+            nc.scalar.copy(out=pos_words[:, start : start + HALF], in_=pos_ps[:])
 
         def normalise_plane(b, t):
             if t == 0:
@@ -222,121 +259,33 @@ def tile_attentionblock_pa_t_kernel(tc, x, pos_enc, gamma1, beta1, W_qkv, b_qkv,
                 out=a_pl[b][:, t, :], in_=h_pl[b][:, t, :], func=ACT.Silu, bias=shift[b][:, t : t + 1], scale=1.0
             )
 
-        def regroup(b, piece):
-            half, part = divmod(piece, 2)
-            if part == 0:
-                a_grp[b, half] = work.tile([P, HALF, PACK], BF16, name="a_grp", align_bytes=64, bufs=1)
-            cols = slice(piece * PIECE, (piece + 1) * PIECE)
-            if b == BATCH - 1 and piece % 2 == 1:
-                nc.scalar.copy(out=a_grp[b, half][:, part * PIECE : (part + 1) * PIECE, :], in_=a_pl[b][:, :, cols].rearrange("p t w -> p w t"))
-                return
-            nc.gpsimd.tensor_scalar(
-                out=a_grp[b, half][:, part * PIECE : (part + 1) * PIECE, :],
-                in0=a_pl[b][:, :, cols].rearrange("p t w -> p w t"),
-                scalar1=1.0,
-                scalar2=0.0,
-                op0=ALU.mult,
-                op1=ALU.add,
-            )
+        def regroup(b, half):
+            a_grp[b, half] = work.tile([P, HALF, PACK], BF16, name="a_grp", align_bytes=64, bufs=1)
+            parts = 2 if b == LAST else 1
+            width = HALF // parts
+            for part in range(parts):
+                first = half * HALF + part * width
+                grouped = a_grp[b, half][:, part * width : (part + 1) * width, :]
+                planes = a_pl[b][:, :, first : first + width].rearrange("p t w -> p w t")
+                if part == 0:
+                    nc.gpsimd.tensor_scalar(out=grouped, in0=planes, scalar1=1.0, scalar2=0.0, op0=ALU.mult, op1=ALU.add)
+                else:
+                    nc.scalar.copy(out=grouped, in_=planes)
 
         def quantise(b, half):
             if half == 0:
                 a_codes[b] = work.tile([P, TOKENS], U32, name="a_codes", align_bytes=64)
                 a_scales[b] = work.tile([P, TOKENS], U8, name="a_scales", align_bytes=64)
-            cols = slice(half * HALF, (half + 1) * HALF)
+            tokens = slice(half * HALF, (half + 1) * HALF)
             nc.vector.quantize_mx(
-                out=a_codes[b][:, cols].bitcast(FP8X4),
-                scales=a_scales[b][:, cols],
+                out=a_codes[b][:, tokens].bitcast(FP8X4),
+                scales=a_scales[b][:, tokens],
                 in_=a_grp[b, half][:].rearrange("p w t -> p (w t)"),
             )
-
-        def multiply(b, j, acc, w_cols):
-            tokens = slice(j * P, (j + 1) * P)
-            nc.tensor.matmul_mx(
-                out=acc,
-                lhsT=a_codes[b][:, tokens].bitcast(FP8X4),
-                lhsT_scale=a_scales[b][:, tokens],
-                rhs=w_codes[:, w_cols].bitcast(FP8X4),
-                rhs_scale=w_scales[:, w_cols],
-                start=True,
-                stop=True,
-            )
-
-        to_fill, to_drain = [], []
-
-        def fill_free_banks():
-            while to_fill and len(to_drain) < AHEAD:
-                b, half, i = to_fill[0]
-                to_fill.remove(to_fill[0])
-                acc = psum.tile([P, WIDE], F32, name="prod", bufs=AHEAD)
-                if i == 0:
-                    for n in range(HALF_TILES):
-                        multiply(b, half * HALF_TILES + n, acc[:, n * NARROW : (n + 1) * NARROW], slice(WIDE, D_OUT))
-                else:
-                    multiply(b, half * HALF_TILES + i - 1, acc[:], slice(0, WIDE))
-                prod[b, half, i] = acc
-                to_drain.append((b, half, i))
-
-        def drain():
-            b, half, i = to_drain[0]
-            to_drain.remove(to_drain[0])
-            if half == 0 and i == 0:
-                out_sb[b] = work.tile([P, TILES, D_OUT], F32, name="out_sb")
-            if i == 0:
-                tiles = slice(half * HALF_TILES, (half + 1) * HALF_TILES)
-                nc.vector.tensor_tensor(
-                    out=out_sb[b][:, tiles, WIDE:D_OUT],
-                    in0=prod[b, half, i][:].rearrange("p (n c) -> p n c", c=NARROW),
-                    in1=bias_bc[:, WIDE:D_OUT].unsqueeze(1).to_broadcast([P, HALF_TILES, NARROW]),
-                    op=ALU.add,
-                )
-            else:
-                j = half * HALF_TILES + i - 1
-                nc.vector.tensor_tensor(
-                    out=out_sb[b][:, j, 0:WIDE], in0=prod[b, half, i][:], in1=bias_bc[:, 0:WIDE], op=ALU.add
-                )
-                step = STORE_TILES if (b, j // STORE_TILES) != (BATCH - 1, TILES // STORE_TILES - 1) else 1
-                if j % step == step - 1:
-                    done = slice(j + 1 - step, j + 1)
-                    nc.sync.dma_start(
-                        out=out[b, :, :].rearrange("(p j) c -> p j c", j=TILES)[:, done, :], in_=out_sb[b][:, done, :]
-                    )
-
-        pos_t = const.tile([P, PAIR, TOKENS, PAIR], BF16)
-        pos_words = pos_t[:].rearrange("p u w e -> p (u w e)").bitcast(F32)
-        nat_words = pos_nat[:].rearrange("p j d -> p (j d)").bitcast(F32)
-
-        def place_pos(k):
-            u, half = divmod(k, 2)
-            pos_ps = psum.tile([P, HALF], F32, name="pos_ps", tag="prod", bufs=AHEAD)
-            for n in range(HALF_TILES):
-                first = (half * HALF_TILES + n) * WORDS
-                nc.tensor.transpose(pos_ps[:, n * P : (n + 1) * P], nat_words[:, first + u : first + WORDS : PAIR], ident_f[:])
-            nc.scalar.copy(out=pos_words[:, k * HALF : (k + 1) * HALF], in_=pos_ps[:])
-
-        for t in range(PACK):
-            transpose_plane(0, t)
-        means(0)
-        vector_stats(0, 0)
-        vector_stats(0, 1)
-        scale_of(0, 0)
-        place_pos(0)
-        place_pos(1)
-        shift_of(0, 0)
-        place_pos(2)
-        place_pos(3)
-        scale_of(0, 1)
-        shift_of(0, 1)
-        for t in range(PACK):
-            token_sums(1, t)
 
         w_grp = const.tile([P, D_OUT, PACK], BF16, align_bytes=64)
         w_codes = const.tile([P, D_OUT], U32, align_bytes=64)
         w_scales = const.tile([P, D_OUT], U8, align_bytes=64)
-
-        nc.gpsimd.tensor_scalar(
-            out=w_grp[:], in0=w_raw[:].rearrange("p t n -> p n t"), scalar1=1.0, scalar2=0.0, op0=ALU.mult, op1=ALU.add
-        )
 
         def quantise_weights():
             for w_cols in (slice(0, WIDE), slice(WIDE, D_OUT)):
@@ -346,15 +295,129 @@ def tile_attentionblock_pa_t_kernel(tc, x, pos_enc, gamma1, beta1, W_qkv, b_qkv,
                     in_=w_grp[:, w_cols, :].rearrange("p n t -> p (n t)"),
                 )
 
-        DL = 1
-        RG = lambda b, i: 4 * b + 4 + i if b else (3, 3, 5, 5)[i]
-        KQ = lambda b, h: 4 * b + 6 + 2 * h if b else (5, 7)[h]
-        DR = lambda k: 0 if k < 6 else 2 + k % 2
-        WQ = 4
-        for quarter in range(BATCH * QUARTERS + DRAIN_LAG + 3):
+        to_fill, to_drain, prod, turned = [], [], {}, {}
+        out_sb, finished, unstored = {}, set(), {}
+
+        def products_of(b, half):
+            wide = [(b, half, half * HALF_TILES + n) for n in range(HALF_TILES)]
+            if is_turned(b, half):
+                return [(b, half, "turned")] + wide[:2] + [(b, half, "back")] + wide[2:]
+            return [(b, half, "narrow")] + wide
+
+        def multiply(acc, stationary, stationary_scales, m_cols, moving, moving_scales, n_cols):
+            nc.tensor.matmul_mx(
+                out=acc,
+                lhsT=stationary[:, m_cols].bitcast(FP8X4),
+                lhsT_scale=stationary_scales[:, m_cols],
+                rhs=moving[:, n_cols].bitcast(FP8X4),
+                rhs_scale=moving_scales[:, n_cols],
+                start=True,
+                stop=True,
+            )
+
+        def fill_free_banks():
+            while to_fill and len(to_drain) < BANKS:
+                b, half, what = to_fill[0]
+                if what == "back" and (b, half) not in turned:
+                    return
+                to_fill.remove(to_fill[0])
+                acc = psum.tile([P, WIDE], F32, name="prod", bufs=BANKS)
+                a_op, w_op = (a_codes[b], a_scales[b]), (w_codes, w_scales)
+                if what == "turned":
+                    multiply(acc[:], *w_op, slice(WIDE, D_OUT), *a_op, slice(half * HALF, (half + 1) * HALF))
+                elif what == "back":
+                    for n in range(HALF_TILES):
+                        cols = slice(n * P, (n + 1) * P)
+                        nc.tensor.transpose(acc[:, cols], turned[b, half][:, cols], ident_f[:])
+                elif what == "narrow":
+                    for n in range(HALF_TILES):
+                        j = half * HALF_TILES + n
+                        cols = slice(n * NARROW, (n + 1) * NARROW)
+                        multiply(acc[:, cols], *a_op, slice(j * P, (j + 1) * P), *w_op, slice(WIDE, D_OUT))
+                else:
+                    multiply(acc[:], *a_op, slice(what * P, (what + 1) * P), *w_op, slice(0, WIDE))
+                prod[b, half, what] = acc
+                to_drain.append((b, half, what))
+
+        def next_filled():
+            b, half, what = to_drain[0]
+            to_drain.remove(to_drain[0])
+            if b not in out_sb:
+                out_sb[b] = work.tile([P, TILES, D_OUT], F32, name="out_sb")
+                cuts = list(range(0, TILES, STORE_TILES)) + ([TILES - 1] if b == LAST else []) + [TILES]
+                unstored[b] = [slice(first, end) for first, end in zip(cuts[:-1], cuts[1:])]
+            return b, half, what
+
+        def narrow_columns(b, half):
+            return out_sb[b][:, half * HALF_TILES : (half + 1) * HALF_TILES, WIDE:D_OUT]
+
+        def store_finished(b):
+            while unstored[b]:
+                tiles = unstored[b][0]
+                if not all((b, j) in finished and (b, j // HALF_TILES, "narrow") in finished for j in range(tiles.start, tiles.stop)):
+                    return
+                unstored[b].remove(tiles)
+                nc.sync.dma_start(out=natural(out[b, :, :])[:, tiles, :], in_=out_sb[b][:, tiles, :])
+
+        def drain_on_scalar():
+            b, half, what = next_filled()
+            acc = prod[b, half, what]
+            if what == "turned":
+                turned[b, half] = work.tile([P, HALF], F32, name="turned")
+                nc.scalar.activation(
+                    out=turned[b, half][:], in_=acc[:], func=ACT.Identity, bias=bias_col[:], scale=1.0
+                )
+            else:
+                nc.scalar.copy(out=narrow_columns(b, half), in_=acc[:].rearrange("p (n c) -> p n c", c=NARROW))
+                finished.add((b, half, "narrow"))
+                store_finished(b)
+
+        def drain_on_vector():
+            b, half, what = next_filled()
+            acc = prod[b, half, what]
+            if what == "narrow":
+                nc.vector.tensor_tensor(
+                    out=narrow_columns(b, half),
+                    in0=acc[:].rearrange("p (n c) -> p n c", c=NARROW),
+                    in1=bias_bc[:, WIDE:D_OUT].unsqueeze(1).to_broadcast([P, HALF_TILES, NARROW]),
+                    op=ALU.add,
+                )
+                finished.add((b, half, "narrow"))
+            else:
+                nc.vector.tensor_tensor(out=out_sb[b][:, what, 0:WIDE], in0=acc[:], in1=bias_bc[:, 0:WIDE], op=ALU.add)
+                finished.add((b, what))
+            store_finished(b)
+
+        def scalar_is_next():
+            return to_drain and to_drain[0][2] in ("turned", "back")
+
+        for t in range(PACK):
+            transpose_plane(0, t)
+        start_stats(0)
+        vector_stats(0)
+        vector_stats(1)
+        scale_of(0, 0)
+        place_pos(0, 0)
+        place_pos(0, 1)
+        shift_of(0, 0)
+        place_pos(1, 0)
+        place_pos(1, 1)
+        scale_of(0, 1)
+        shift_of(0, 1)
+        for t in range(PACK):
+            own_products(t)
+        nc.gpsimd.tensor_scalar(
+            out=w_grp[:], in0=w_raw[:].rearrange("p t n -> p n t"), scalar1=1.0, scalar2=0.0, op0=ALU.mult, op1=ALU.add
+        )
+
+        for quarter in range(quantise_at(LAST, 1) + 3):
             b, q = divmod(quarter, QUARTERS)
-            if q == 0 and 1 <= b and b + 1 < BATCH:
+            if q == 0 and 2 <= b + 1 < BATCH:
                 means(b + 1)
+            if quarter == BIAS_ROUND * QUARTERS:
+                nc.scalar.copy(out=bias_col[:], in_=sums[b + 1][:, PACK, 0:1])
+            if scalar_is_next() and quantise_at(*to_drain[0][:2]) < quarter:
+                drain_on_scalar()
             if b < BATCH:
                 normalise_plane(b, q)
                 swish(b, q)
@@ -363,38 +426,36 @@ def tile_attentionblock_pa_t_kernel(tc, x, pos_enc, gamma1, beta1, W_qkv, b_qkv,
                 if b >= 1:
                     centred_squares(b + 1, q)
             if quarter == 0:
-                means(1)
-            if quarter == 1:
-                own_means(1, 0)
-            if quarter == 2:
-                own_means(1, 1)
+                start_stats(1)
+            if quarter in (1, 2):
+                own_means(quarter - 1)
             if quarter == 3:
-                own_stats(1, 0)
-                own_stats(1, 1)
+                for pair in range(2):
+                    own_variances(pair)
+                    scale_of(1, pair)
                 quantise_weights()
                 shift_of(1, 0)
             if b + 2 < BATCH:
                 token_sums(b + 2, q)
-            for rb in range(BATCH):
-                for half in range(2):
-                    if KQ(rb, half) == quarter:
-                        quantise(rb, half)
-                        to_fill.extend([(rb, half, i) for i in range(BANKS_PER_HALF)])
-            for rb in range(BATCH):
-                for piece in range(QUARTERS):
-                    if RG(rb, piece) == quarter:
-                        regroup(rb, piece)
+            halves = [(rb, half) for rb in range(BATCH) for half in range(2)]
+            for rb, half in halves:
+                if quantise_at(rb, half) == quarter:
+                    quantise(rb, half)
+                    to_fill.extend(products_of(rb, half))
+            for rb, half in halves:
+                if regroup_at(rb, half) == quarter:
+                    regroup(rb, half)
             if q == 1:
-                if b >= 1 and b + 1 < BATCH:
+                if 2 <= b + 1 < BATCH:
                     scale_of(b + 1, 0)
                 if 1 <= b < BATCH:
                     shift_of(b, 1)
-            if q == 3:
-                if 1 <= b and b + 1 < BATCH:
-                    scale_of(b + 1, 1)
-                    shift_of(b + 1, 0)
+            if q == 3 and 2 <= b + 1 < BATCH:
+                scale_of(b + 1, 1)
+                shift_of(b + 1, 0)
             fill_free_banks()
-            for i in range(DR(quarter)):
-                if to_drain and KQ(*to_drain[0][:2]) + DL <= quarter:
-                    drain()
-                    fill_free_banks()
+            if quarter >= FIRST_DRAIN:
+                for n in range(2 + quarter % 2):
+                    if to_drain and not scalar_is_next() and quantise_at(*to_drain[0][:2]) < quarter:
+                        drain_on_vector()
+                        fill_free_banks()

@@ -47,7 +47,7 @@ def quantise_at(b, half):
 
 
 def is_turned(b, half):
-    return (LAST - 2, 0) <= (b, half) < (LAST, 1)
+    return LAST - 2 <= b < LAST
 
 
 def tile_attentionblock_pa_t_kernel(tc, x, pos_enc, gamma1, beta1, W_qkv, b_qkv, out):
@@ -71,7 +71,9 @@ def tile_attentionblock_pa_t_kernel(tc, x, pos_enc, gamma1, beta1, W_qkv, b_qkv,
         nc.scalar.dma_start(out=gamma[:], in_=gamma1[0, :, :].rearrange("a (p t) -> (a p) t", t=PACK))
         nc.scalar.dma_start(out=beta[:], in_=beta1[0, :, :].rearrange("a (p t) -> (a p) t", t=PACK))
         pos_nat = const.tile([P, TILES, D_IN], BF16)
-        nc.sync.dma_start(out=pos_nat[:], in_=natural(pos_enc[0, :, :]))
+        for half in range(2):
+            tiles = slice(half * HALF_TILES, (half + 1) * HALF_TILES)
+            nc.sync.dma_start(out=pos_nat[:, tiles, :], in_=natural(pos_enc[0, :, :])[:, tiles, :])
         x_own = const.tile([P, TILES, LEAD + D_IN], BF16, align_bytes=64)
         nc.gpsimd.memset(x_own[:, :, 0:LEAD], 1.0)
         x_nat[1] = x_own[:, :, LEAD : LEAD + D_IN]
@@ -121,15 +123,29 @@ def tile_attentionblock_pa_t_kernel(tc, x, pos_enc, gamma1, beta1, W_qkv, b_qkv,
             for j in range(TILES):
                 nc.tensor.transpose(x_t[b, t][:, j * P : (j + 1) * P], x_nat[b][:, j, t:D_IN:PACK], ident[:])
 
+        def transpose_words(bank, nat, q):
+            u, half = divmod(q, 2)
+            words = nat[:].rearrange("p j d -> p (j d)").bitcast(F32)
+            for n in range(HALF_TILES):
+                first = (half * HALF_TILES + n) * WORDS
+                nc.tensor.transpose(bank[:, n * P : (n + 1) * P], words[:, first + u : first + WORDS : PAIR], ident_f[:])
+
+        def pieces(b, q):
+            if b > 0:
+                return [(q, slice(0, TOKENS), x_t[b, q][:])]
+            u, half = divmod(q, 2)
+            values = x_t[0, q][:].bitcast(BF16).rearrange("p (w e) -> p w e", e=PAIR)
+            tokens = slice(half * HALF, (half + 1) * HALF)
+            return [(u * PAIR + e, tokens, values[:, :, e]) for e in range(PAIR)]
+
         def vector_stats(pair):
             mean_var[pair] = small.tile([P, PAIR, 2], F32, name="mean_var")
+            parts = [small.tile([P, 2, 6], F32, name="parts%d" % t) for t in range(PAIR)]
+            for half in range(2):
+                for t, tokens, values in pieces(0, 2 * pair + half):
+                    nc.vector.bn_stats(out=parts[t % PAIR][:, half, :], in_=values)
             for t in range(PAIR):
-                parts = small.tile([P, 2, 6], F32, name="parts")
-                for half in range(2):
-                    nc.vector.bn_stats(
-                        out=parts[:, half, :], in_=x_t[0, pair * PAIR + t][:, half * HALF : (half + 1) * HALF]
-                    )
-                nc.vector.bn_aggr(out=mean_var[pair][:, t, :], in_=parts[:].rearrange("p h s -> p (h s)"))
+                nc.vector.bn_aggr(out=mean_var[pair][:, t, :], in_=parts[t][:].rearrange("p h s -> p (h s)"))
 
         def own_products(t):
             if t % PAIR == 0:
@@ -208,8 +224,13 @@ def tile_attentionblock_pa_t_kernel(tc, x, pos_enc, gamma1, beta1, W_qkv, b_qkv,
                 )
                 nc.scalar.activation(out=neg_mean[b][:, planes], in_=mean_var[pair][:, :, 0], func=ACT.Copy, scale=-1.0)
             if b >= 2:
-                nc.scalar.activation(
-                    out=var_eps[b][:, planes], in_=sum_sq[b][:, planes], func=ACT.Copy, scale=1.0 / TOKENS, bias=EPS
+                nc.gpsimd.tensor_scalar(
+                    out=var_eps[b][:, planes],
+                    in0=sum_sq[b][:, planes],
+                    scalar1=1.0 / TOKENS,
+                    scalar2=EPS,
+                    op0=ALU.mult,
+                    op1=ALU.add,
                 )
             rstd = small.tile([P, PAIR], F32, name="rstd")
             nc.gpsimd.tensor_tensor(out=rstd[:], in0=var_eps[b][:, planes], in1=minus_half[:], op=ALU.pow)
@@ -228,36 +249,32 @@ def tile_attentionblock_pa_t_kernel(tc, x, pos_enc, gamma1, beta1, W_qkv, b_qkv,
         h_pl, a_pl, a_grp, a_codes, a_scales = {}, {}, {}, {}, {}
         pos_t = const.tile([P, PAIR, TOKENS, PAIR], BF16)
         pos_words = pos_t[:].rearrange("p u w e -> p (u w e)").bitcast(F32)
-        nat_words = pos_nat[:].rearrange("p j d -> p (j d)").bitcast(F32)
 
-        def place_pos(u, half):
+        def place_pos(q):
             pos_ps = psum.tile([P, HALF], F32, name="pos_ps", tag="prod", bufs=BANKS)
-            for n in range(HALF_TILES):
-                first = (half * HALF_TILES + n) * WORDS
-                nc.tensor.transpose(
-                    pos_ps[:, n * P : (n + 1) * P], nat_words[:, first + u : first + WORDS : PAIR], ident_f[:]
-                )
-            start = u * TOKENS + half * HALF
-            nc.scalar.copy(out=pos_words[:, start : start + HALF], in_=pos_ps[:])
+            transpose_words(pos_ps, pos_nat, q)
+            nc.scalar.copy(out=pos_words[:, q * HALF : (q + 1) * HALF], in_=pos_ps[:])
 
-        def normalise_plane(b, t):
-            if t == 0:
+        def normalise(b, q):
+            if q == 0:
                 h_pl[b] = work.tile([P, PACK, TOKENS], F32, name="h_pl")
-            nc.vector.scalar_tensor_tensor(
-                out=h_pl[b][:, t, :],
-                in0=x_t[b, t][:],
-                scalar=scale[b][:, t : t + 1],
-                in1=pos_t[:, t // PAIR, :, t % PAIR],
-                op0=ALU.mult,
-                op1=ALU.add,
-            )
+            for t, tokens, values in pieces(b, q):
+                nc.vector.scalar_tensor_tensor(
+                    out=h_pl[b][:, t, tokens],
+                    in0=values,
+                    scalar=scale[b][:, t : t + 1],
+                    in1=pos_t[:, t // PAIR, tokens, t % PAIR],
+                    op0=ALU.mult,
+                    op1=ALU.add,
+                )
 
-        def swish(b, t):
-            if t == 0:
+        def swish(b, q):
+            if q == 0:
                 a_pl[b] = work.tile([P, PACK, TOKENS], BF16, name="a_pl")
-            nc.scalar.activation(
-                out=a_pl[b][:, t, :], in_=h_pl[b][:, t, :], func=ACT.Silu, bias=shift[b][:, t : t + 1], scale=1.0
-            )
+            for t, tokens, values in pieces(b, q):
+                nc.scalar.activation(
+                    out=a_pl[b][:, t, tokens], in_=h_pl[b][:, t, tokens], func=ACT.Silu, bias=shift[b][:, t : t + 1], scale=1.0
+                )
 
         def regroup(b, half):
             a_grp[b, half] = work.tile([P, HALF, PACK], BF16, name="a_grp", align_bytes=64, bufs=1)
@@ -391,17 +408,18 @@ def tile_attentionblock_pa_t_kernel(tc, x, pos_enc, gamma1, beta1, W_qkv, b_qkv,
         def scalar_is_next():
             return to_drain and to_drain[0][2] in ("turned", "back")
 
-        for t in range(PACK):
-            transpose_plane(0, t)
+        for q in range(QUARTERS):
+            x_t[0, q] = psum.tile([P, HALF], F32, name="x_words", tag="x_t%d" % q)
+            transpose_words(x_t[0, q], x_nat[0], q)
         start_stats(0)
         vector_stats(0)
         vector_stats(1)
         scale_of(0, 0)
-        place_pos(0, 0)
-        place_pos(0, 1)
+        place_pos(0)
+        place_pos(1)
         shift_of(0, 0)
-        place_pos(1, 0)
-        place_pos(1, 1)
+        place_pos(2)
+        place_pos(3)
         scale_of(0, 1)
         shift_of(0, 1)
         for t in range(PACK):
@@ -419,7 +437,7 @@ def tile_attentionblock_pa_t_kernel(tc, x, pos_enc, gamma1, beta1, W_qkv, b_qkv,
             if scalar_is_next() and quantise_at(*to_drain[0][:2]) < quarter:
                 drain_on_scalar()
             if b < BATCH:
-                normalise_plane(b, q)
+                normalise(b, q)
                 swish(b, q)
             if b + 1 < BATCH:
                 transpose_plane(b + 1, q)

@@ -47,7 +47,7 @@ def quantise_at(b, half):
 
 
 def is_turned(b, half):
-    return LAST - 2 <= b < LAST
+    return LAST - 2 <= b < LAST or (b in (2, 3) and half == 1)
 
 
 def tile_attentionblock_pa_t_kernel(tc, x, pos_enc, gamma1, beta1, W_qkv, b_qkv, out):
@@ -453,8 +453,6 @@ def tile_attentionblock_pa_t_kernel(tc, x, pos_enc, gamma1, beta1, W_qkv, b_qkv,
                     scale_of(1, pair)
                 quantise_weights()
                 shift_of(1, 0)
-            if b + 2 < BATCH:
-                token_sums(b + 2, q)
             halves = [(rb, half) for rb in range(BATCH) for half in range(2)]
             for rb, half in halves:
                 if quantise_at(rb, half) == quarter:
@@ -472,6 +470,8 @@ def tile_attentionblock_pa_t_kernel(tc, x, pos_enc, gamma1, beta1, W_qkv, b_qkv,
                 scale_of(b + 1, 1)
                 shift_of(b + 1, 0)
             fill_free_banks()
+            if b + 2 < BATCH:
+                token_sums(b + 2, q)
             if quarter >= FIRST_DRAIN:
                 for n in range(2 + quarter % 2):
                     if to_drain and not scalar_is_next() and quantise_at(*to_drain[0][:2]) < quarter:

from contextlib import ExitStack

import concourse.masks as masks
import concourse.mybir as mybir

F32 = mybir.dt.float32
BF16 = mybir.dt.bfloat16
U32 = mybir.dt.uint32
U8 = mybir.dt.uint8
FP8X4 = mybir.dt.float8_e4m3fn_x4
ACT = mybir.ActivationFunctionType
ALU = mybir.AluOpType

P = 128
PACK = 4
PAIR = PACK // 2
BATCH = 8
TOKENS = 1024
D_IN = P * PACK
D_OUT = 640
TILES = TOKENS // P
HALF = TOKENS // 2
HALF_TILES = TILES // 2
QUARTERS = PACK
WORDS = D_IN // PAIR
WIDE = 512
NARROW = D_OUT - WIDE
BANKS = 3
FIRST_DRAIN = 6
LAST = BATCH - 1
SUM_COLS = 60
LEAD = 16
OWN_COLS = 1 + P
BIAS_ROUND = 3
STORE_TILES = 2
EPS = 1e-5

FLOPS = 2 * BATCH * TOKENS * D_IN * D_OUT


def regroup_at(b, half):
    return QUARTERS * (b + 1) + 2 * half - (b == 0)


def quantise_at(b, half):
    return regroup_at(b, half) + 2


def is_turned(b, half):
    return LAST - 2 <= b < LAST or (b in (2, 3) and half == 1)


def tile_attentionblock_pa_t_kernel(tc, x, pos_enc, gamma1, beta1, W_qkv, b_qkv, out):
    nc = tc.nc
    with ExitStack() as ctx:
        const = ctx.enter_context(tc.tile_pool(name="const", bufs=1))
        work = ctx.enter_context(tc.tile_pool(name="work", bufs=2))
        small = ctx.enter_context(tc.tile_pool(name="small", bufs=4))
        psum = ctx.enter_context(tc.psum_pool(name="psum", bufs=1))
        ctx.enter_context(tc.manual_schedule())

        def natural(dram):
            return dram.rearrange("(p j) d -> p j d", j=TILES)

        x_nat = {0: const.tile([P, TILES, D_IN], BF16, name="x0")}
        for half in range(2):
            tiles = slice(half * HALF_TILES, (half + 1) * HALF_TILES)
            nc.sync.dma_start(out=x_nat[0][:, tiles, :], in_=natural(x[0, :, :])[:, tiles, :])
        gamma = const.tile([P, PACK], BF16)
        beta = const.tile([P, PACK], BF16)
        nc.scalar.dma_start(out=gamma[:], in_=gamma1[0, :, :].rearrange("a (p t) -> (a p) t", t=PACK))
        nc.scalar.dma_start(out=beta[:], in_=beta1[0, :, :].rearrange("a (p t) -> (a p) t", t=PACK))
        pos_nat = const.tile([P, TILES, D_IN], BF16)
        for half in range(2):
            tiles = slice(half * HALF_TILES, (half + 1) * HALF_TILES)
            nc.sync.dma_start(out=pos_nat[:, tiles, :], in_=natural(pos_enc[0, :, :])[:, tiles, :])
        x_own = const.tile([P, TILES, LEAD + D_IN], BF16, align_bytes=64)
        nc.gpsimd.memset(x_own[:, :, 0:LEAD], 1.0)
        x_nat[1] = x_own[:, :, LEAD : LEAD + D_IN]
        nc.sync.dma_start(out=x_nat[1], in_=natural(x[1, :, :]))
        w_raw = const.tile([P, PACK, D_OUT], BF16)
        bias_bc = const.tile([P, D_OUT], BF16)

        def load_x(b):
            x_nat[b] = const.tile([P, TILES, D_IN], BF16, name="x%d" % b)
            nc.sync.dma_start(out=x_nat[b][:], in_=natural(x[b, :, :]))

        nc.sync.dma_start(out=w_raw[:], in_=W_qkv.rearrange("(p t) n -> p t n", t=PACK))
        for b in range(2, 5):
            load_x(b)
        nc.sync.dma_start(out=bias_bc[:], in_=b_qkv.partition_broadcast(P))
        for b in range(5, BATCH):
            load_x(b)

        ident = const.tile([P, P], BF16)
        masks.make_identity(nc, ident[:])
        bias_col = const.tile([P, 1], F32)
        ident_f = const.tile([P, P], F32)
        masks.make_identity(nc, ident_f[:])
        ones = const.tile([P, SUM_COLS], BF16)
        nc.vector.memset(ones[:], 1.0)
        minus_half = const.tile([P, PAIR], F32)
        nc.vector.memset(minus_half[:], -0.5)
        warm = const.tile([P, 1], F32)
        nc.vector.memset(warm[:], 0.0)
        nc.scalar.activation(out=warm[:], in_=warm[:], func=ACT.Silu)

        x_t, sums, own, mean_var, mean_sq = {}, {}, {}, {}, {}
        neg_mean, sum_sq, var_eps, scale, shift = {}, {}, {}, {}, {}

        def planes_of(pair):
            return slice(pair * PAIR, (pair + 1) * PAIR)

        def start_stats(b):
            neg_mean[b] = small.tile([P, PACK], F32, name="neg_mean")
            sum_sq[b] = small.tile([P, PACK], F32, name="sum_sq")
            var_eps[b] = small.tile([P, PACK], F32, name="var_eps")
            scale[b] = small.tile([P, PACK], F32, name="scale")
            shift[b] = small.tile([P, PACK], F32, name="shift")

        def transpose_plane(b, t):
            x_t[b, t] = psum.tile([P, TOKENS], BF16, name="x_t", tag="x_t%d" % t)
            for j in range(TILES):
                nc.tensor.transpose(x_t[b, t][:, j * P : (j + 1) * P], x_nat[b][:, j, t:D_IN:PACK], ident[:])

        def transpose_words(bank, nat, q):
            u, half = divmod(q, 2)
            words = nat[:].rearrange("p j d -> p (j d)").bitcast(F32)
            for n in range(HALF_TILES):
                first = (half * HALF_TILES + n) * WORDS
                nc.tensor.transpose(bank[:, n * P : (n + 1) * P], words[:, first + u : first + WORDS : PAIR], ident_f[:])

        def pieces(b, q):
            if b > 0:
                return [(q, slice(0, TOKENS), x_t[b, q][:])]
            u, half = divmod(q, 2)
            values = x_t[0, q][:].bitcast(BF16).rearrange("p (w e) -> p w e", e=PAIR)
            tokens = slice(half * HALF, (half + 1) * HALF)
            return [(u * PAIR + e, tokens, values[:, :, e]) for e in range(PAIR)]

        def vector_stats(pair):
            mean_var[pair] = small.tile([P, PAIR, 2], F32, name="mean_var")
            parts = [small.tile([P, 2, 6], F32, name="parts%d" % t) for t in range(PAIR)]
            for half in range(2):
                for t, tokens, values in pieces(0, 2 * pair + half):
                    nc.vector.bn_stats(out=parts[t % PAIR][:, half, :], in_=values)
            for t in range(PAIR):
                nc.vector.bn_aggr(out=mean_var[pair][:, t, :], in_=parts[t][:].rearrange("p h s -> p (h s)"))

        def own_products(t):
            if t % PAIR == 0:
                own[t // PAIR] = psum.tile([P, PAIR, OWN_COLS], F32, name="own", tag="prod", bufs=BANKS)
            for j in range(TILES):
                nc.tensor.matmul(
                    out=own[t // PAIR][:, t % PAIR, :],
                    lhsT=x_nat[1][:, j, t:D_IN:PACK],
                    rhs=x_own[:, j, LEAD - PACK + t : LEAD + D_IN : PACK],
                    start=(j == 0),
                    stop=(j == TILES - 1),
                )

        def own_means(pair):
            nc.scalar.activation(
                out=neg_mean[1][:, planes_of(pair)], in_=own[pair][:, :, 0], func=ACT.Copy, scale=-1.0 / TOKENS
            )
            mean_sq[pair] = small.tile([P, PAIR], F32, name="mean_sq")
            nc.scalar.activation(out=mean_sq[pair][:], in_=neg_mean[1][:, planes_of(pair)], func=ACT.Square)

        def own_variances(pair):
            squares = small.tile([P, PAIR], F32, name="squares")
            for t in range(PAIR):
                unused = work.tile([P, P], F32, name="unused_products")
                nc.vector.scalar_tensor_tensor(
                    out=unused[:],
                    in0=own[pair][:, t, 1:OWN_COLS],
                    scalar=1.0 / TOKENS,
                    in1=ident_f[:],
                    op0=ALU.mult,
                    op1=ALU.mult,
                    accum_out=squares[:, t : t + 1],
                )
            var = small.tile([P, PAIR], F32, name="var")
            nc.vector.tensor_tensor(out=var[:], in0=squares[:], in1=mean_sq[pair][:], op=ALU.subtract)
            nc.vector.tensor_scalar(
                out=var_eps[1][:, planes_of(pair)], in0=var[:], scalar1=0.0, scalar2=EPS, op0=ALU.max, op1=ALU.add
            )

        def token_sums(b, t):
            if t == 0:
                sums[b] = psum.tile([P, PACK + 1, SUM_COLS], F32, name="sums")
                if b == BIAS_ROUND + 1:
                    nc.tensor.matmul(
                        out=sums[b][:, PACK, 0:2], lhsT=bias_bc[:, WIDE:D_OUT], rhs=ident[:, 0:2], start=True, stop=True
                    )
            for j in range(TILES):
                nc.tensor.matmul(
                    out=sums[b][:, t, :],
                    lhsT=x_nat[b][:, j, t:D_IN:PACK],
                    rhs=ones[:],
                    start=(j == 0),
                    stop=(j == TILES - 1),
                )

        def means(b):
            start_stats(b)
            nc.scalar.activation(out=neg_mean[b][:], in_=sums[b][:, 0:PACK, 0], func=ACT.Copy, scale=-1.0 / TOKENS)

        def centred_squares(b, t):
            unused = work.tile([P, TOKENS], BF16, name="unused")
            nc.scalar.activation(
                out=unused[:],
                in_=x_t[b, t][:],
                func=ACT.Square,
                bias=neg_mean[b][:, t : t + 1],
                scale=1.0,
                accum_out=sum_sq[b][:, t : t + 1],
            )

        def scale_of(b, pair):
            planes = planes_of(pair)
            if b == 0:
                nc.scalar.activation(
                    out=var_eps[b][:, planes], in_=mean_var[pair][:, :, 1], func=ACT.Copy, scale=1.0, bias=EPS
                )
                nc.scalar.activation(out=neg_mean[b][:, planes], in_=mean_var[pair][:, :, 0], func=ACT.Copy, scale=-1.0)
            if b >= 2:
                nc.gpsimd.tensor_scalar(
                    out=var_eps[b][:, planes],
                    in0=sum_sq[b][:, planes],
                    scalar1=1.0 / TOKENS,
                    scalar2=EPS,
                    op0=ALU.mult,
                    op1=ALU.add,
                )
            rstd = small.tile([P, PAIR], F32, name="rstd")
            nc.gpsimd.tensor_tensor(out=rstd[:], in0=var_eps[b][:, planes], in1=minus_half[:], op=ALU.pow)
            nc.gpsimd.tensor_tensor(out=scale[b][:, planes], in0=rstd[:], in1=gamma[:, planes], op=ALU.mult)

        def shift_of(b, pair):
            for t in range(pair * PAIR, (pair + 1) * PAIR):
                nc.scalar.activation(
                    out=shift[b][:, t : t + 1],
                    in_=scale[b][:, t : t + 1],
                    func=ACT.Identity,
                    scale=neg_mean[b][:, t : t + 1],
                    bias=beta[:, t : t + 1],
                )

        h_pl, a_pl, a_grp, a_codes, a_scales = {}, {}, {}, {}, {}
        pos_t = const.tile([P, PAIR, TOKENS, PAIR], BF16)
        pos_words = pos_t[:].rearrange("p u w e -> p (u w e)").bitcast(F32)

        def place_pos(q):
            pos_ps = psum.tile([P, HALF], F32, name="pos_ps", tag="prod", bufs=BANKS)
            transpose_words(pos_ps, pos_nat, q)
            nc.scalar.copy(out=pos_words[:, q * HALF : (q + 1) * HALF], in_=pos_ps[:])

        def normalise(b, q):
            if q == 0:
                h_pl[b] = work.tile([P, PACK, TOKENS], F32, name="h_pl")
            for t, tokens, values in pieces(b, q):
                nc.vector.scalar_tensor_tensor(
                    out=h_pl[b][:, t, tokens],
                    in0=values,
                    scalar=scale[b][:, t : t + 1],
                    in1=pos_t[:, t // PAIR, tokens, t % PAIR],
                    op0=ALU.mult,
                    op1=ALU.add,
                )

        def swish(b, q):
            if q == 0:
                a_pl[b] = work.tile([P, PACK, TOKENS], BF16, name="a_pl")
            for t, tokens, values in pieces(b, q):
                nc.scalar.activation(
                    out=a_pl[b][:, t, tokens], in_=h_pl[b][:, t, tokens], func=ACT.Silu, bias=shift[b][:, t : t + 1], scale=1.0
                )

        def regroup(b, half):
            a_grp[b, half] = work.tile([P, HALF, PACK], BF16, name="a_grp", align_bytes=64, bufs=1)
            parts = 2 if b == LAST else 1
            width = HALF // parts
            for part in range(parts):
                first = half * HALF + part * width
                grouped = a_grp[b, half][:, part * width : (part + 1) * width, :]
                planes = a_pl[b][:, :, first : first + width].rearrange("p t w -> p w t")
                if part == 0:
                    nc.gpsimd.tensor_scalar(out=grouped, in0=planes, scalar1=1.0, scalar2=0.0, op0=ALU.mult, op1=ALU.add)
                else:
                    nc.scalar.copy(out=grouped, in_=planes)

        def quantise(b, half):
            if half == 0:
                a_codes[b] = work.tile([P, TOKENS], U32, name="a_codes", align_bytes=64)
                a_scales[b] = work.tile([P, TOKENS], U8, name="a_scales", align_bytes=64)
            tokens = slice(half * HALF, (half + 1) * HALF)
            nc.vector.quantize_mx(
                out=a_codes[b][:, tokens].bitcast(FP8X4),
                scales=a_scales[b][:, tokens],
                in_=a_grp[b, half][:].rearrange("p w t -> p (w t)"),
            )

        w_grp = const.tile([P, D_OUT, PACK], BF16, align_bytes=64)
        w_codes = const.tile([P, D_OUT], U32, align_bytes=64)
        w_scales = const.tile([P, D_OUT], U8, align_bytes=64)

        def quantise_weights():
            for w_cols in (slice(0, WIDE), slice(WIDE, D_OUT)):
                nc.vector.quantize_mx(
                    out=w_codes[:, w_cols].bitcast(FP8X4),
                    scales=w_scales[:, w_cols],
                    in_=w_grp[:, w_cols, :].rearrange("p n t -> p (n t)"),
                )

        to_fill, to_drain, prod, turned = [], [], {}, {}
        out_sb, finished, unstored = {}, set(), {}

        def products_of(b, half):
            wide = [(b, half, half * HALF_TILES + n) for n in range(HALF_TILES)]
            if is_turned(b, half):
                return [(b, half, "turned")] + wide[:2] + [(b, half, "back")] + wide[2:]
            return [(b, half, "narrow")] + wide

        def multiply(acc, stationary, stationary_scales, m_cols, moving, moving_scales, n_cols):
            nc.tensor.matmul_mx(
                out=acc,
                lhsT=stationary[:, m_cols].bitcast(FP8X4),
                lhsT_scale=stationary_scales[:, m_cols],
                rhs=moving[:, n_cols].bitcast(FP8X4),
                rhs_scale=moving_scales[:, n_cols],
                start=True,
                stop=True,
            )

        def fill_free_banks():
            while to_fill and len(to_drain) < BANKS:
                b, half, what = to_fill[0]
                if what == "back" and (b, half) not in turned:
                    return
                to_fill.remove(to_fill[0])
                acc = psum.tile([P, WIDE], F32, name="prod", bufs=BANKS)
                a_op, w_op = (a_codes[b], a_scales[b]), (w_codes, w_scales)
                if what == "turned":
                    multiply(acc[:], *w_op, slice(WIDE, D_OUT), *a_op, slice(half * HALF, (half + 1) * HALF))
                elif what == "back":
                    for n in range(HALF_TILES):
                        cols = slice(n * P, (n + 1) * P)
                        nc.tensor.transpose(acc[:, cols], turned[b, half][:, cols], ident_f[:])
                elif what == "narrow":
                    for n in range(HALF_TILES):
                        j = half * HALF_TILES + n
                        cols = slice(n * NARROW, (n + 1) * NARROW)
                        multiply(acc[:, cols], *a_op, slice(j * P, (j + 1) * P), *w_op, slice(WIDE, D_OUT))
                else:
                    multiply(acc[:], *a_op, slice(what * P, (what + 1) * P), *w_op, slice(0, WIDE))
                prod[b, half, what] = acc
                to_drain.append((b, half, what))

        def next_filled():
            b, half, what = to_drain[0]
            to_drain.remove(to_drain[0])
            if b not in out_sb:
                out_sb[b] = work.tile([P, TILES, D_OUT], F32, name="out_sb")
                cuts = list(range(0, TILES, STORE_TILES)) + ([TILES - 1] if b == LAST else []) + [TILES]
                unstored[b] = [slice(first, end) for first, end in zip(cuts[:-1], cuts[1:])]
            return b, half, what

        def narrow_columns(b, half):
            return out_sb[b][:, half * HALF_TILES : (half + 1) * HALF_TILES, WIDE:D_OUT]

        def store_finished(b):
            while unstored[b]:
                tiles = unstored[b][0]
                if not all((b, j) in finished and (b, j // HALF_TILES, "narrow") in finished for j in range(tiles.start, tiles.stop)):
                    return
                unstored[b].remove(tiles)
                nc.sync.dma_start(out=natural(out[b, :, :])[:, tiles, :], in_=out_sb[b][:, tiles, :])

        def drain_on_scalar():
            b, half, what = next_filled()
            acc = prod[b, half, what]
            if what == "turned":
                turned[b, half] = work.tile([P, HALF], F32, name="turned")
                nc.scalar.activation(
                    out=turned[b, half][:], in_=acc[:], func=ACT.Identity, bias=bias_col[:], scale=1.0
                )
            else:
                nc.scalar.copy(out=narrow_columns(b, half), in_=acc[:].rearrange("p (n c) -> p n c", c=NARROW))
                finished.add((b, half, "narrow"))
                store_finished(b)

        def drain_on_vector():
            b, half, what = next_filled()
            acc = prod[b, half, what]
            if what == "narrow":
                nc.vector.tensor_tensor(
                    out=narrow_columns(b, half),
                    in0=acc[:].rearrange("p (n c) -> p n c", c=NARROW),
                    in1=bias_bc[:, WIDE:D_OUT].unsqueeze(1).to_broadcast([P, HALF_TILES, NARROW]),
                    op=ALU.add,
                )
                finished.add((b, half, "narrow"))
            else:
                nc.vector.tensor_tensor(out=out_sb[b][:, what, 0:WIDE], in0=acc[:], in1=bias_bc[:, 0:WIDE], op=ALU.add)
                finished.add((b, what))
            store_finished(b)

        def scalar_is_next():
            return to_drain and to_drain[0][2] in ("turned", "back")

        for q in range(QUARTERS):
            x_t[0, q] = psum.tile([P, HALF], F32, name="x_words", tag="x_t%d" % q)
            transpose_words(x_t[0, q], x_nat[0], q)
        start_stats(0)
        vector_stats(0)
        vector_stats(1)
        scale_of(0, 0)
        place_pos(0)
        place_pos(1)
        shift_of(0, 0)
        place_pos(2)
        place_pos(3)
        scale_of(0, 1)
        shift_of(0, 1)
        for t in range(PACK):
            own_products(t)
        nc.gpsimd.tensor_scalar(
            out=w_grp[:], in0=w_raw[:].rearrange("p t n -> p n t"), scalar1=1.0, scalar2=0.0, op0=ALU.mult, op1=ALU.add
        )

        for quarter in range(quantise_at(LAST, 1) + 3):
            b, q = divmod(quarter, QUARTERS)
            if q == 0 and 2 <= b + 1 < BATCH:
                means(b + 1)
            if quarter == BIAS_ROUND * QUARTERS:
                nc.scalar.copy(out=bias_col[:], in_=sums[b + 1][:, PACK, 0:1])
            if scalar_is_next() and quantise_at(*to_drain[0][:2]) < quarter:
                drain_on_scalar()
            if b < BATCH:
                normalise(b, q)
                swish(b, q)
            if b + 1 < BATCH:
                transpose_plane(b + 1, q)
                if b >= 1:
                    centred_squares(b + 1, q)
            if quarter == 0:
                start_stats(1)
            if quarter in (1, 2):
                own_means(quarter - 1)
            if quarter == 3:
                for pair in range(2):
                    own_variances(pair)
                    scale_of(1, pair)
                quantise_weights()
                shift_of(1, 0)
            halves = [(rb, half) for rb in range(BATCH) for half in range(2)]
            for rb, half in halves:
                if quantise_at(rb, half) == quarter:
                    quantise(rb, half)
                    to_fill.extend(products_of(rb, half))
            for rb, half in halves:
                if regroup_at(rb, half) == quarter:
                    regroup(rb, half)
            if q == 1:
                if 2 <= b + 1 < BATCH:
                    scale_of(b + 1, 0)
                if 1 <= b < BATCH:
                    shift_of(b, 1)
            if q == 3 and 2 <= b + 1 < BATCH:
                scale_of(b + 1, 1)
                shift_of(b + 1, 0)
            fill_free_banks()
            if b + 2 < BATCH:
                token_sums(b + 2, q)
            if quarter >= FIRST_DRAIN:
                for n in range(2 + quarter % 2):
                    if to_drain and not scalar_is_next() and quantise_at(*to_drain[0][:2]) < quarter:
                        drain_on_vector()
                        fill_free_banks()
